import numpy as np
import ml_dtypes


def mxq(x, axis, fmt="e4m3"):
    dtype, down = {"e4m3": (ml_dtypes.float8_e4m3fn, 7), "e5m2": (ml_dtypes.float8_e5m2, 14)}[fmt]
    v = np.moveaxis(np.asarray(x, np.float32).astype(ml_dtypes.bfloat16).astype(np.float64), axis, -1)
    blocks = v.reshape(v.shape[:-1] + (-1, 32))
    amax = np.abs(blocks).max(-1, keepdims=True)
    byte = np.maximum(np.where(amax > 0, np.frexp(amax)[1] - 1 + 127, 0) - down, 1)
    scale = np.exp2(byte - 127.0)
    codes = (blocks / scale).astype(np.float32).astype(dtype).astype(np.float64)
    return np.moveaxis((codes * scale).reshape(v.shape), -1, axis)


WIDE = False


def mx_kscale(k):
    if not WIDE:
        return np.ones(k)
    levels = np.array([10, -10, 5, -5, 0])
    if k % 512:
        return np.exp2(np.random.permutation(np.resize(levels, k // 32))).repeat(32)
    a = np.empty((k // 512, 16))
    for p in range(k // 512):
        a[p, :8] = np.random.permutation(np.resize(levels, 8))
        for g in range(8):
            far = levels[np.abs(levels - a[p, g]) >= 10]
            a[p, g + 8] = far[np.random.randint(len(far))]
    return np.exp2(a.ravel()).repeat(32)


BF16 = ml_dtypes.bfloat16


def bf(x):
    return np.asarray(x, np.float32).astype(BF16)


def f64(x):
    return np.asarray(x).astype(np.float64)


E2M1 = np.array([0.0, 0.5, 1.0, 1.5, 2.0, 3.0, 4.0, 6.0, -0.0, -0.5, -1.0, -1.5, -2.0, -3.0, -4.0, -6.0])


def pack_weight(w, fmt):
    k, n = w.shape
    w = f64(bf(w)).reshape(k // 32, 32, n)
    amax = np.abs(w).max(1)
    if fmt == "e4m3":
        byte = np.frexp(amax)[1] - 1 + 127 - 7
    else:
        mant, ex = np.frexp(amax / 6.0)
        byte = np.where(mant > 0.5, ex, ex - 1) + 127
    byte = np.clip(np.where(amax > 0, byte, 1), 1, 254)
    scaled = (w * np.exp2(127.0 - byte)[:, None, :]).reshape(k, n).astype(np.float32)
    by_word = np.ascontiguousarray(scaled.reshape(k // 512, 128, 4, n).transpose(0, 1, 3, 2))
    if fmt == "e4m3":
        words = by_word.astype(ml_dtypes.float8_e4m3fn).view(np.uint8)
    else:
        c = by_word.astype(ml_dtypes.float4_e2m1fn).view(np.uint8) & 0xF
        words = c[..., 0::2] | (c[..., 1::2] << 4)
    return np.ascontiguousarray(words), np.ascontiguousarray(byte.astype(np.uint8).reshape(k // 512, 16, n))


def unpack_weight(words, scales, fmt):
    g, p, n, _ = words.shape
    if fmt == "e4m3":
        vals = np.ascontiguousarray(words).view(ml_dtypes.float8_e4m3fn).astype(np.float64)
    else:
        nib = np.empty((g, p, n, 4), np.uint8)
        nib[..., 0::2] = words & 0xF
        nib[..., 1::2] = words >> 4
        vals = E2M1[nib]
    vals = vals * np.repeat(np.exp2(scales.astype(np.float64) - 127.0), 8, axis=1)[..., None]
    return vals.transpose(0, 1, 3, 2).reshape(g * 512, n)
def pack4(w):
    words, scales = pack_weight(w, "e2m1")
    return words.reshape(words.shape[0], 128, -1), scales


def unpack4(words, scales):
    return unpack_weight(words.reshape(words.shape[0], 128, -1, 2), scales, "e2m1")


N, IN_DIM, HID, OUT_DIM = 1024, 1024, 512, 256
CAT = 3 * HID


def log_softmax(v):
    d = v - v.max(-1, keepdims=True)
    return d - np.log(np.exp(d).sum(-1, keepdims=True))


def draw0():
    s, t = mx_kscale(HID), mx_kscale(CAT)
    ta, tb, tc = t[:HID], t[HID:2 * HID], t[2 * HID:]
    u1 = bf(np.maximum(np.random.standard_normal((N, HID)) * 2.0, 0.0) * s)
    W2_1_words, W2_1_scales = pack4(np.random.standard_normal((HID, HID)) * 0.5 / np.sqrt(HID) / s[:, None] * tc)
    b2_1 = bf(np.random.standard_normal(HID) * 0.3 * tc)
    h = bf(np.random.standard_normal((N, HID)) * ta)
    h1 = bf(np.random.standard_normal((N, HID)) * 0.8 * tb)
    W_out_words, W_out_scales = pack4(np.random.standard_normal((CAT, OUT_DIM)) * 2.0 / np.sqrt(CAT) / t[:, None])
    b_out = bf(np.random.standard_normal(OUT_DIM) * 0.3)
    return {"u1": u1,
            "W2_1_words": W2_1_words,
            "W2_1_scales": W2_1_scales,
            "b2_1": b2_1,
            "h": h,
            "h1": h1,
            "W_out_words": W_out_words,
            "W_out_scales": W_out_scales,
            "b_out": b_out}


def core(u1, W2_1_words, W2_1_scales, b2_1, h, h1, W_out_words, W_out_scales, b_out):
    h2 = (mxq(f64(u1), 1, "e4m3") @ unpack4(W2_1_words, W2_1_scales)) + f64(b2_1)
    cat = np.concatenate([f64(h), f64(h1), h2], axis=-1)
    logits = (mxq(cat, 1, "e4m3") @ unpack4(W_out_words, W_out_scales)) + f64(b_out)
    return log_softmax(logits)


def e4m3fn_bytes(y):
    return np.clip(np.asarray(y, np.float64), -448.0, 448.0).astype(np.float32).astype(ml_dtypes.float8_e4m3fn).view(np.uint8)


def e4m3fn_values(b):
    return np.asarray(b, np.uint8).view(ml_dtypes.float8_e4m3fn).astype(np.float64)


def setup_inputs():
    d = draw0()
    x0 = np.asarray(d['u1']).astype(np.float64)
    s = (np.max(np.abs(x0), axis=(0,), keepdims=True) / 448.0).astype(np.float32)
    out = {}
    for k, v in d.items():
        if k == 'u1':
            out['u1_bytes'] = e4m3fn_bytes(x0 / s.astype(np.float64))
            out['u1_scale'] = s
        else:
            out[k] = v
    return out


def reference(u1_bytes, u1_scale, W2_1_words, W2_1_scales, b2_1, h, h1, W_out_words, W_out_scales, b_out):
    return core(e4m3fn_values(u1_bytes) * u1_scale.astype(np.float64), W2_1_words, W2_1_scales, b2_1, h, h1, W_out_words, W_out_scales, b_out)

@@ -1,0 +1,377 @@
+import math
+from contextlib import ExitStack
+
+import concourse.mybir as mybir
+from concourse.masks import make_identity
+
+FLOPS = 2 * 1024 * 512 * 512 + 2 * 1024 * 1536 * 256
+
+F32 = mybir.dt.float32
+BF16 = mybir.dt.bfloat16
+I32 = mybir.dt.int32
+U32 = mybir.dt.uint32
+U8 = mybir.dt.uint8
+FP8 = mybir.dt.float8_e4m3fn
+FP8X4 = mybir.dt.float8_e4m3fn_x4
+FP4X4 = mybir.dt.float4_e2m1fn_x4
+ADD = mybir.AluOpType.add
+SUB = mybir.AluOpType.subtract
+MULT = mybir.AluOpType.mult
+MAX = mybir.AluOpType.max
+AX = mybir.AxisListType.X
+POW = mybir.AluOpType.pow
+EXP = mybir.ActivationFunctionType.Exp
+LN = mybir.ActivationFunctionType.Ln
+IDENT = mybir.ActivationFunctionType.Identity
+
+LOG_MID = 2.0 ** 0.0625
+
+P = 128
+NODES, HID, CLS = 1024, 512, 256
+NB = NODES // P
+NP = NB // 2
+
+
+def tile_gin_pc_w4_kernel(
+    tc, u1_bytes, u1_scale, w2_words, w2_scales, b2_1, h, h1, wo_words, wo_scales, b_out, out
+):
+    nc = tc.nc
+    with ExitStack() as ctx:
+        keep = ctx.enter_context(tc.tile_pool(name="keep", bufs=1))
+        tr_pool = ctx.enter_context(tc.psum_pool(name="tr_pool", bufs=4))
+        h2_pool = ctx.enter_context(tc.psum_pool(name="h2_pool", bufs=2))
+        lg_pool = ctx.enter_context(tc.psum_pool(name="lg_pool", bufs=2))
+        ctx.enter_context(tc.manual_schedule())
+
+        def sb(shape, dtype, name):
+            return keep.tile(shape, dtype, name=name, align_bytes=64)
+
+        scale_col = sb([P, 4], F32, "scale_col")
+        bo_col = sb([P, 2], BF16, "bo_col")
+        b2_col = sb([P, 4], BF16, "b2_col")
+        u_raw = [sb([P, 2, HID], U8, f"u_raw{i}") for i in range(NP)]
+        h_sb = [sb([P, 2, HID], BF16, f"h_sb{i}") for i in range(NP)]
+        g_sb = [sb([P, 2, HID], BF16, f"g_sb{i}") for i in range(NP)]
+        w2_in = sb([P, 2 * HID], U8, "w2_in")
+        w2_perm = sb([P, 2 * HID], U8, "w2_perm")
+        w2s_in = sb([P, HID], U8, "w2s_in")
+        w2s_perm = sb([P, HID], U8, "w2s_perm")
+        wo = sb([P, 3, 2 * CLS], U8, "wo")
+        wos = sb([P, 3, CLS], U8, "wos")
+        ident = sb([P, P], F32, "ident")
+        scale_all = sb([P, HID], F32, "scale_all")
+        bo_all = sb([P, CLS], BF16, "bo_all")
+        u_val = [sb([P, 2, HID], BF16, f"u_val{i}") for i in range(NP)]
+        u_grp = [sb([P, 256, 4], BF16, f"u_grp{i}") for i in range(NP)]
+        hg_grp = [sb([P, 2, 256, 4], BF16, f"hg_grp{i}") for i in range(NP)]
+        h2_grp = [sb([P, 256, 4], BF16, f"h2_grp{i}") for i in range(NP)]
+        u_codes = [sb([P, 256], U32, f"u_codes{i}") for i in range(NP)]
+        u_scl = [sb([P, 256], U8, f"u_scl{i}") for i in range(NP)]
+        hg_codes = [sb([P, 512], U32, f"hg_codes{i}") for i in range(NP)]
+        hg_scl = [sb([P, 512], U8, f"hg_scl{i}") for i in range(NP)]
+        h2_codes = [sb([P, 256], U32, f"h2_codes{i}") for i in range(NP)]
+        h2_scl = [sb([P, 256], U8, f"h2_scl{i}") for i in range(NP)]
+        logits = [sb([P, 2, CLS], F32, f"logits{i}") for i in range(NP)]
+        junk = sb([P, CLS], F32, "junk")
+        nmax = sb([P, NB], F32, "nmax")
+        ssum = sb([P, NB], F32, "ssum")
+        lns = sb([P, NB], F32, "lns")
+        shift = sb([P, NB], F32, "shift")
+        res = [sb([P, 2, CLS], F32, f"res{i}") for i in range(NP)]
+        warm = sb([P, 1], F32, "warm")
+        root_exp = sb([P, 2], F32, "root_exp")
+        minus_one = sb([P, 2], F32, "minus_one")
+
+        u_hbm = u1_bytes.rearrange("(p b) k -> p b k", b=NB)
+        h_hbm = h.rearrange("(p b) k -> p b k", b=NB)
+        g_hbm = h1.rearrange("(p b) k -> p b k", b=NB)
+        o_hbm = out.rearrange("(p b) c -> p b c", b=NB)
+
+        def load_u(i):
+            nc.sync.dma_start(out=u_raw[i][:], in_=u_hbm[:, 2 * i : 2 * i + 2, :])
+
+        def load_h(i):
+            nc.sync.dma_start(out=h_sb[i][:], in_=h_hbm[:, 2 * i : 2 * i + 2, :])
+
+        def load_g(i):
+            nc.sync.dma_start(out=g_sb[i][:], in_=g_hbm[:, 2 * i : 2 * i + 2, :])
+
+        nc.gpsimd.memset(w2s_in[:].bitcast(I32), 0)
+        nc.gpsimd.memset(warm[:], 0.0)
+        make_identity(nc, ident[:])
+        nc.gpsimd.memset(root_exp[:], 1.0 / 64.0)
+        nc.gpsimd.memset(minus_one[:], -1.0)
+        nc.gpsimd.memset(wos[:].rearrange("p g n -> p (g n)").bitcast(I32), 0)
+
+        nc.sync.dma_start(out=scale_col[:], in_=u1_scale.rearrange("o (p j) -> p (o j)", j=4))
+        load_u(0)
+        nc.sync.dma_start(out=w2_in[:], in_=w2_words[0])
+        w2s_hbm = w2_scales[0].rearrange("(q r) n -> r q n", r=4)
+        for r in range(4):
+            nc.sync.dma_start(out=w2s_in[r:P:32, :].bitcast(I32), in_=w2s_hbm[r].bitcast(I32))
+        load_h(0)
+        load_u(1)
+        load_g(0)
+        nc.sync.dma_start(out=b2_col[:], in_=b2_1.rearrange("(p t) -> p t", t=4))
+        nc.sync.dma_start(out=bo_col[:], in_=b_out.rearrange("(p t) -> p t", t=2))
+        load_h(1)
+        load_u(2)
+        load_g(1)
+        load_u(3)
+        nc.sync.dma_start(out=wo[:], in_=wo_words.rearrange("g p n -> p g n"))
+        wos_hbm = wo_scales.rearrange("g (q r) n -> r q g n", r=4)
+        for r in range(4):
+            nc.sync.dma_start(out=wos[r:P:32, :, :].bitcast(I32), in_=wos_hbm[r].bitcast(I32))
+        load_h(2)
+        load_g(2)
+        load_h(3)
+        load_g(3)
+
+        nc.scalar.activation(out=warm[:], in_=warm[:], func=EXP)
+
+        def spread_scale():
+            bank = tr_pool.tile([P, 4, P], F32, name="bank", tag="tr")
+            for j in range(4):
+                nc.tensor.transpose(bank[:, j, :], scale_col[:, j : j + 1].to_broadcast([P, P]), ident[:])
+            nc.scalar.copy(
+                out=scale_all[:].rearrange("p (n j) -> p n j", j=4), in_=bank[:].rearrange("p j n -> p n j")
+            )
+
+        def spread_b_out():
+            bank = tr_pool.tile([P, P], F32, name="bank", tag="tr")
+            nc.tensor.transpose(bank[:], bo_col[:].bitcast(F32).to_broadcast([P, P]), ident[:])
+            nc.scalar.copy(out=bo_all[:].bitcast(F32), in_=bank[:])
+
+        def permute_w2_words():
+            nc.vector.tensor_copy(
+                out=w2_perm[:].rearrange("p (t m b) -> p t m b", t=4, b=2),
+                in_=w2_in[:].rearrange("p (m t b) -> p t m b", t=4, b=2),
+            )
+
+        def permute_w2_scales():
+            nc.vector.tensor_copy(
+                out=w2s_perm[:].rearrange("p (t m) -> p t m", t=4),
+                in_=w2s_in[:].rearrange("p (m t) -> p t m", t=4),
+            )
+
+        def widen(i):
+            for b in range(2):
+                nc.vector.tensor_tensor(
+                    out=u_val[i][:, b, :], in0=u_raw[i][:, b, :].bitcast(FP8), in1=scale_all[:], op=MULT
+                )
+
+        def turn(src, dst):
+            bank = tr_pool.tile([P, 2, 2, P], F32, name="bank", tag="tr")
+            for b in range(2):
+                words = src[:, b, :].bitcast(F32)
+                for e in range(2):
+                    nc.tensor.transpose(bank[:, b, e, :], words[:, e : HID // 2 : 2], ident[:])
+            nc.scalar.copy(
+                out=dst.rearrange("p (b n) t -> p b n t", b=2).bitcast(F32),
+                in_=bank[:].rearrange("p b e n -> p b n e"),
+            )
+
+        def quantize(codes, scl, grp):
+            nc.vector.quantize_mx(out=codes[:].bitcast(FP8X4), scales=scl[:], in_=grp)
+
+        def quantize_u(i):
+            quantize(u_codes[i], u_scl[i], u_grp[i][:].rearrange("p n t -> p (n t)"))
+
+        def quantize_hg(i):
+            quantize(hg_codes[i], hg_scl[i], hg_grp[i][:].rearrange("p s n t -> p (s n t)"))
+
+        def quantize_h2(i):
+            quantize(h2_codes[i], h2_scl[i], h2_grp[i][:].rearrange("p n t -> p (n t)"))
+
+        h2_ps = {}
+
+        def matmul_h2(i):
+            for b in range(2):
+                bank = h2_pool.tile([P, 4, P], F32, name="h2_bank", tag="h2")
+                h2_ps[i, b] = bank
+                nodes = slice(b * P, (b + 1) * P)
+                for t in range(4):
+                    nc.tensor.matmul_mx(
+                        out=bank[:, t, :],
+                        lhsT=w2_perm[:, 2 * P * t : 2 * P * (t + 1)].bitcast(FP4X4),
+                        lhsT_scale=w2s_perm[:, P * t : P * (t + 1)],
+                        rhs=u_codes[i][:, nodes].bitcast(FP8X4),
+                        rhs_scale=u_scl[i][:, nodes],
+                        start=True,
+                        stop=True,
+                    )
+
+        def bias_h2(i):
+            for b in range(2):
+                nc.vector.tensor_tensor(
+                    out=h2_grp[i][:, b * P : (b + 1) * P, :],
+                    in0=h2_ps[i, b][:].rearrange("p t n -> p n t"),
+                    in1=b2_col[:].unsqueeze(1).to_broadcast([P, P, 4]),
+                    op=ADD,
+                )
+
+        lg_ps = {}
+
+        def matmul_out(i):
+            bank = lg_pool.tile([P, 2, CLS], F32, name="lg_bank", tag="lg")
+            lg_ps[i] = bank
+            for b in range(2):
+                for c in range(2):
+                    cls = slice(c * P, (c + 1) * P)
+                    for g in range(3):
+                        if g < 2:
+                            n0 = g * 256 + b * P
+                            codes, scl = hg_codes[i], hg_scl[i]
+                        else:
+                            n0 = b * P
+                            codes, scl = h2_codes[i], h2_scl[i]
+                        nc.tensor.matmul_mx(
+                            out=bank[:, b, cls],
+                            lhsT=codes[:, n0 : n0 + P].bitcast(FP8X4),
+                            lhsT_scale=scl[:, n0 : n0 + P],
+                            rhs=wo[:, g, 2 * P * c : 2 * P * (c + 1)].bitcast(FP4X4),
+                            rhs_scale=wos[:, g, cls],
+                            start=(g == 0),
+                            stop=(g == 2),
+                        )
+
+        def bias_out(i, blocks=slice(0, 2)):
+            k = blocks.stop - blocks.start
+            nc.vector.tensor_tensor(
+                out=logits[i][:, blocks, :],
+                in0=lg_ps[i][:, blocks, :],
+                in1=bo_all[:].unsqueeze(1).to_broadcast([P, k, CLS]),
+                op=ADD,
+            )
+
+        def row_max(i, blocks=slice(0, 2)):
+            nc.vector.tensor_reduce(
+                out=nmax[:, 2 * i + blocks.start : 2 * i + blocks.stop],
+                in_=logits[i][:, blocks, :],
+                axis=AX,
+                op=MAX,
+                negate=True,
+            )
+
+        def exp_sum(i, blocks=slice(0, 2)):
+            for b in range(blocks.start, blocks.stop):
+                n = 2 * i + b
+                nc.scalar.activation(
+                    out=junk[:],
+                    in_=logits[i][:, b, :],
+                    func=EXP,
+                    bias=nmax[:, n : n + 1],
+                    accum_out=ssum[:, n : n + 1],
+                )
+
+        def log_sum(b0, b1):
+            nc.scalar.activation(out=lns[:, b0:b1], in_=ssum[:, b0:b1], func=LN)
+
+        def make_shift(b0, b1):
+            nc.vector.tensor_tensor(out=shift[:, b0:b1], in0=nmax[:, b0:b1], in1=lns[:, b0:b1], op=SUB)
+
+        def gpsimd_shift(i):
+            cols = slice(2 * i, 2 * i + 2)
+            root = sb([P, 2], F32, f"root{i}")
+            den = sb([P, 2], F32, f"den{i}")
+            z = sb([P, 2], F32, f"z{i}")
+            w = sb([P, 2], F32, f"w{i}")
+            q = sb([P, 2], F32, f"q{i}")
+            g = nc.gpsimd
+            g.tensor_tensor(out=root[:], in0=ssum[:, cols], in1=root_exp[:], op=POW)
+            g.tensor_scalar(out=den[:], in0=root[:], scalar1=LOG_MID, scalar2=None, op0=ADD)
+            g.tensor_tensor(out=den[:], in0=den[:], in1=minus_one[:], op=POW)
+            g.tensor_scalar(out=root[:], in0=root[:], scalar1=-LOG_MID, scalar2=None, op0=ADD)
+            g.tensor_tensor(out=z[:], in0=root[:], in1=den[:], op=MULT)
+            g.tensor_tensor(out=w[:], in0=z[:], in1=z[:], op=MULT)
+            g.tensor_scalar(out=q[:], in0=w[:], scalar1=1.0 / 5.0, scalar2=1.0 / 3.0, op0=MULT, op1=ADD)
+            g.tensor_tensor(out=q[:], in0=q[:], in1=w[:], op=MULT)
+            g.tensor_tensor(out=q[:], in0=q[:], in1=z[:], op=MULT)
+            g.tensor_tensor(out=q[:], in0=q[:], in1=z[:], op=ADD)
+            g.tensor_scalar(
+                out=q[:], in0=q[:], scalar1=-128.0, scalar2=-64.0 * math.log(LOG_MID), op0=MULT, op1=ADD
+            )
+            g.tensor_tensor(out=shift[:, cols], in0=q[:], in1=nmax[:, cols], op=ADD)
+
+        def finish(i, b, on_scalar):
+            n = 2 * i + b
+            if on_scalar:
+                nc.scalar.activation(
+                    out=res[i][:, b, :], in_=logits[i][:, b, :], func=IDENT, bias=shift[:, n : n + 1]
+                )
+            else:
+                nc.vector.tensor_scalar(
+                    out=res[i][:, b, :], in0=logits[i][:, b, :], scalar1=shift[:, n : n + 1], scalar2=None, op0=ADD
+                )
+
+        def store(i):
+            nc.sync.dma_start(out=o_hbm[:, 2 * i : 2 * i + 2, :], in_=res[i][:])
+
+        def turn_u(i):
+            turn(u_val[i], u_grp[i][:])
+
+        def turn_hg(i):
+            turn(h_sb[i], hg_grp[i][:, 0])
+            turn(g_sb[i], hg_grp[i][:, 1])
+
+        def turn_h(i):
+            turn(h_sb[i], hg_grp[i][:, 0])
+
+        def turn_g(i):
+            turn(g_sb[i], hg_grp[i][:, 1])
+
+        spread_scale()
+        permute_w2_words()
+        widen(0)
+        turn_u(0)
+        permute_w2_scales()
+        turn_h(0)
+        widen(1)
+        turn_g(0)
+        turn_u(1)
+        quantize_u(0)
+        matmul_h2(0)
+        spread_b_out()
+        widen(2)
+        turn_u(2)
+        turn_h(1)
+        quantize_hg(0)
+        quantize_u(1)
+        bias_h2(0)
+        matmul_h2(1)
+        turn_g(1)
+        widen(3)
+        turn_u(3)
+        quantize_h2(0)
+        matmul_out(0)
+        for i in range(1, NP):
+            if i + 1 < NP:
+                quantize_u(i + 1)
+            bias_h2(i)
+            if i + 1 < NP:
+                matmul_h2(i + 1)
+                turn_hg(i + 1)
+            quantize_hg(i)
+            bias_out(i - 1)
+            quantize_h2(i)
+            matmul_out(i)
+            row_max(i - 1)
+            exp_sum(i - 1)
+            if i < 3:
+                gpsimd_shift(i - 1)
+        last = NP - 1
+        for b in range(2):
+            blk = slice(b, b + 1)
+            bias_out(last, blk)
+            row_max(last, blk)
+            exp_sum(last, blk)
+        for i in range(2):
+            finish(i, 0, False)
+            finish(i, 1, False)
+            store(i)
+        log_sum(4, 8)
+        make_shift(4, 8)
+        for i in (2, 3):
+            finish(i, 0, False)
+            finish(i, 1, True)
+            store(i)

@@ -49,9 +49,14 @@ def tile_gin_pc_w4_kernel(
         scale_col = sb([P, 4], F32, "scale_col")
         bo_col = sb([P, 2], BF16, "bo_col")
         b2_col = sb([P, 4], BF16, "b2_col")
-        u_raw = [sb([P, 2, HID], U8, f"u_raw{i}") for i in range(NP)]
-        h_sb = [sb([P, 2, HID], BF16, f"h_sb{i}") for i in range(NP)]
-        g_sb = [sb([P, 2, HID], BF16, f"g_sb{i}") for i in range(NP)]
+        chunks = [(0, 2), (2, 4), (4, 8)]
+        u_raw = [sb([P, b1 - b0, HID], U8, f"u_raw{b0}") for b0, b1 in chunks]
+        h_sb = [sb([P, b1 - b0, HID], BF16, f"h_sb{b0}") for b0, b1 in chunks]
+        g_sb = [sb([P, b1 - b0, HID], BF16, f"g_sb{b0}") for b0, b1 in chunks]
+
+        def block(tiles, n):
+            c = min(n // 2, 2)
+            return tiles[c][:, n - chunks[c][0], :]
         w2_in = sb([P, 2 * HID], U8, "w2_in")
         w2_perm = sb([P, 2 * HID], U8, "w2_perm")
         w2s_in = sb([P, HID], U8, "w2s_in")
@@ -88,13 +93,13 @@ def tile_gin_pc_w4_kernel(
         o_hbm = out.rearrange("(p b) c -> p b c", b=NB)
 
         def load_u(i):
-            nc.sync.dma_start(out=u_raw[i][:], in_=u_hbm[:, 2 * i : 2 * i + 2, :])
+            nc.sync.dma_start(out=u_raw[i][:], in_=u_hbm[:, chunks[i][0] : chunks[i][1], :])
 
         def load_h(i):
-            nc.sync.dma_start(out=h_sb[i][:], in_=h_hbm[:, 2 * i : 2 * i + 2, :])
+            nc.sync.dma_start(out=h_sb[i][:], in_=h_hbm[:, chunks[i][0] : chunks[i][1], :])
 
         def load_g(i):
-            nc.sync.dma_start(out=g_sb[i][:], in_=g_hbm[:, 2 * i : 2 * i + 2, :])
+            nc.sync.dma_start(out=g_sb[i][:], in_=g_hbm[:, chunks[i][0] : chunks[i][1], :])
 
         nc.gpsimd.memset(w2s_in[:].bitcast(I32), 0)
         nc.gpsimd.memset(warm[:], 0.0)
@@ -106,31 +111,33 @@ def tile_gin_pc_w4_kernel(
         nc.sync.dma_start(out=scale_col[:], in_=u1_scale.rearrange("o (p j) -> p (o j)", j=4))
         load_u(0)
         nc.sync.dma_start(out=w2_in[:], in_=w2_words[0])
+        load_h(0)
         w2s_hbm = w2_scales[0].rearrange("(q r) n -> r q n", r=4)
         for r in range(4):
             nc.sync.dma_start(out=w2s_in[r:P:32, :].bitcast(I32), in_=w2s_hbm[r].bitcast(I32))
-        load_h(0)
         load_u(1)
         load_g(0)
-        nc.sync.dma_start(out=b2_col[:], in_=b2_1.rearrange("(p t) -> p t", t=4))
-        nc.sync.dma_start(out=bo_col[:], in_=b_out.rearrange("(p t) -> p t", t=2))
         load_h(1)
+        nc.sync.dma_start(out=b2_col[:], in_=b2_1.rearrange("(p t) -> p t", t=4))
         load_u(2)
         load_g(1)
-        load_u(3)
+        nc.sync.dma_start(out=bo_col[:], in_=b_out.rearrange("(p t) -> p t", t=2))
         nc.sync.dma_start(out=wo[:], in_=wo_words.rearrange("g p n -> p g n"))
         wos_hbm = wo_scales.rearrange("g (q r) n -> r q g n", r=4)
         for r in range(4):
             nc.sync.dma_start(out=wos[r:P:32, :, :].bitcast(I32), in_=wos_hbm[r].bitcast(I32))
         load_h(2)
         load_g(2)
-        load_h(3)
-        load_g(3)
 
         nc.scalar.activation(out=warm[:], in_=warm[:], func=EXP)
 
+        def dummies(bank, k):
+            for n in range(k):
+                nc.tensor.matmul(bank, lhsT=ident[:], rhs=ident[:], start=True, stop=True)
+
         def spread_scale():
             bank = tr_pool.tile([P, 4, P], F32, name="bank", tag="tr")
+            dummies(bank[:, 0, :], 4)
             for j in range(4):
                 nc.tensor.transpose(bank[:, j, :], scale_col[:, j : j + 1].to_broadcast([P, P]), ident[:])
             nc.scalar.copy(
@@ -157,13 +164,14 @@ def tile_gin_pc_w4_kernel(
         def widen(i):
             for b in range(2):
                 nc.vector.tensor_tensor(
-                    out=u_val[i][:, b, :], in0=u_raw[i][:, b, :].bitcast(FP8), in1=scale_all[:], op=MULT
+                    out=u_val[i][:, b, :], in0=block(u_raw, 2 * i + b).bitcast(FP8), in1=scale_all[:], op=MULT
                 )
 
-        def turn(src, dst):
+        def turn(src, dst, k=1):
             bank = tr_pool.tile([P, 2, 2, P], F32, name="bank", tag="tr")
+            dummies(bank[:, 0, 0, :], k)
             for b in range(2):
-                words = src[:, b, :].bitcast(F32)
+                words = src[b].bitcast(F32)
                 for e in range(2):
                     nc.tensor.transpose(bank[:, b, e, :], words[:, e : HID // 2 : 2], ident[:])
             nc.scalar.copy(
@@ -304,28 +312,39 @@ def tile_gin_pc_w4_kernel(
                     out=res[i][:, b, :], in0=logits[i][:, b, :], scalar1=shift[:, n : n + 1], scalar2=None, op0=ADD
                 )
 
+        def finish_ln(i, b):
+            n = 2 * i + b
+            nc.vector.tensor_scalar(
+                out=res[i][:, b, :],
+                in0=logits[i][:, b, :],
+                scalar1=nmax[:, n : n + 1],
+                scalar2=lns[:, n : n + 1],
+                op0=ADD,
+                op1=SUB,
+            )
+
         def store(i):
             nc.sync.dma_start(out=o_hbm[:, 2 * i : 2 * i + 2, :], in_=res[i][:])
 
         def turn_u(i):
-            turn(u_val[i], u_grp[i][:])
+            turn([u_val[i][:, b, :] for b in range(2)], u_grp[i][:])
 
         def turn_hg(i):
-            turn(h_sb[i], hg_grp[i][:, 0])
-            turn(g_sb[i], hg_grp[i][:, 1])
+            turn([block(h_sb, 2 * i + b) for b in range(2)], hg_grp[i][:, 0])
+            turn([block(g_sb, 2 * i + b) for b in range(2)], hg_grp[i][:, 1])
 
         def turn_h(i):
-            turn(h_sb[i], hg_grp[i][:, 0])
+            turn([block(h_sb, 2 * i + b) for b in range(2)], hg_grp[i][:, 0])
 
         def turn_g(i):
-            turn(g_sb[i], hg_grp[i][:, 1])
+            turn([block(g_sb, 2 * i + b) for b in range(2)], hg_grp[i][:, 1])
 
         spread_scale()
         permute_w2_words()
+        turn_h(0)
         widen(0)
         turn_u(0)
         permute_w2_scales()
-        turn_h(0)
         widen(1)
         turn_g(0)
         turn_u(1)
@@ -370,8 +389,10 @@ def tile_gin_pc_w4_kernel(
             finish(i, 1, False)
             store(i)
         log_sum(4, 8)
+        finish_ln(2, 0)
         make_shift(4, 8)
-        for i in (2, 3):
-            finish(i, 0, False)
-            finish(i, 1, True)
-            store(i)
+        finish(2, 1, True)
+        store(2)
+        finish_ln(3, 0)
+        finish_ln(3, 1)
+        store(3)

@@ -1,4 +1,3 @@
-import math
 from contextlib import ExitStack
 
 import concourse.mybir as mybir
@@ -19,17 +18,16 @@ SUB = mybir.AluOpType.subtract
 MULT = mybir.AluOpType.mult
 MAX = mybir.AluOpType.max
 AX = mybir.AxisListType.X
-POW = mybir.AluOpType.pow
 EXP = mybir.ActivationFunctionType.Exp
 LN = mybir.ActivationFunctionType.Ln
 IDENT = mybir.ActivationFunctionType.Identity
-
-LOG_MID = 2.0 ** 0.0625
 
 P = 128
 NODES, HID, CLS = 1024, 512, 256
 NB = NODES // P
 NP = NB // 2
+BOTH = slice(0, 2)
+LGB = (0, 1)
 
 
 def tile_gin_pc_w4_kernel(
@@ -38,9 +36,10 @@ def tile_gin_pc_w4_kernel(
     nc = tc.nc
     with ExitStack() as ctx:
         keep = ctx.enter_context(tc.tile_pool(name="keep", bufs=1))
-        tr_pool = ctx.enter_context(tc.psum_pool(name="tr_pool", bufs=4))
+        tr_pool = ctx.enter_context(tc.psum_pool(name="tr_pool", bufs=3))
         h2_pool = ctx.enter_context(tc.psum_pool(name="h2_pool", bufs=2))
-        lg_pool = ctx.enter_context(tc.psum_pool(name="lg_pool", bufs=2))
+        lgt_pool = ctx.enter_context(tc.psum_pool(name="lgt_pool", bufs=1))
+        lgb_pool = ctx.enter_context(tc.psum_pool(name="lgb_pool", bufs=2))
         ctx.enter_context(tc.manual_schedule())
 
         def sb(shape, dtype, name):
@@ -48,6 +47,7 @@ def tile_gin_pc_w4_kernel(
 
         scale_col = sb([P, 4], F32, "scale_col")
         bo_col = sb([P, 2], BF16, "bo_col")
+        bo_cls = sb([P, 2], BF16, "bo_cls")
         b2_col = sb([P, 4], BF16, "b2_col")
         chunks = [(0, 2), (2, 4), (4, 8)]
         u_raw = [sb([P, b1 - b0, HID], U8, f"u_raw{b0}") for b0, b1 in chunks]
@@ -57,6 +57,7 @@ def tile_gin_pc_w4_kernel(
         def block(tiles, n):
             c = min(n // 2, 2)
             return tiles[c][:, n - chunks[c][0], :]
+
         w2_in = sb([P, 2 * HID], U8, "w2_in")
         w2_perm = sb([P, 2 * HID], U8, "w2_perm")
         w2s_in = sb([P, HID], U8, "w2s_in")
@@ -64,11 +65,12 @@ def tile_gin_pc_w4_kernel(
         wo = sb([P, 3, 2 * CLS], U8, "wo")
         wos = sb([P, 3, CLS], U8, "wos")
         ident = sb([P, P], F32, "ident")
-        scale_all = sb([P, HID], F32, "scale_all")
+        scale_all = sb([P, 2, HID], F32, "scale_all")
         bo_all = sb([P, CLS], BF16, "bo_all")
         u_val = [sb([P, 2, HID], BF16, f"u_val{i}") for i in range(NP)]
         u_grp = [sb([P, 256, 4], BF16, f"u_grp{i}") for i in range(NP)]
         hg_grp = [sb([P, 2, 256, 4], BF16, f"hg_grp{i}") for i in range(NP)]
+        h2_flat = [sb([P, 2, 4, P], BF16, f"h2_flat{i}") for i in range(NP)]
         h2_grp = [sb([P, 256, 4], BF16, f"h2_grp{i}") for i in range(NP)]
         u_codes = [sb([P, 256], U32, f"u_codes{i}") for i in range(NP)]
         u_scl = [sb([P, 256], U8, f"u_scl{i}") for i in range(NP)]
@@ -77,15 +79,13 @@ def tile_gin_pc_w4_kernel(
         h2_codes = [sb([P, 256], U32, f"h2_codes{i}") for i in range(NP)]
         h2_scl = [sb([P, 256], U8, f"h2_scl{i}") for i in range(NP)]
         logits = [sb([P, 2, CLS], F32, f"logits{i}") for i in range(NP)]
+        lgt_sb = [sb([P, 2, 256], F32, f"lgt_sb{i}") for i in range(NP)]
         junk = sb([P, CLS], F32, "junk")
         nmax = sb([P, NB], F32, "nmax")
         ssum = sb([P, NB], F32, "ssum")
         lns = sb([P, NB], F32, "lns")
-        shift = sb([P, NB], F32, "shift")
         res = [sb([P, 2, CLS], F32, f"res{i}") for i in range(NP)]
         warm = sb([P, 1], F32, "warm")
-        root_exp = sb([P, 2], F32, "root_exp")
-        minus_one = sb([P, 2], F32, "minus_one")
 
         u_hbm = u1_bytes.rearrange("(p b) k -> p b k", b=NB)
         h_hbm = h.rearrange("(p b) k -> p b k", b=NB)
@@ -104,22 +104,21 @@ def tile_gin_pc_w4_kernel(
         nc.gpsimd.memset(w2s_in[:].bitcast(I32), 0)
         nc.gpsimd.memset(warm[:], 0.0)
         make_identity(nc, ident[:])
-        nc.gpsimd.memset(root_exp[:], 1.0 / 64.0)
-        nc.gpsimd.memset(minus_one[:], -1.0)
         nc.gpsimd.memset(wos[:].rearrange("p g n -> p (g n)").bitcast(I32), 0)
 
-        nc.sync.dma_start(out=scale_col[:], in_=u1_scale.rearrange("o (p j) -> p (o j)", j=4))
-        load_u(0)
-        nc.sync.dma_start(out=w2_in[:], in_=w2_words[0])
-        load_h(0)
         w2s_hbm = w2_scales[0].rearrange("(q r) n -> r q n", r=4)
         for r in range(4):
             nc.sync.dma_start(out=w2s_in[r:P:32, :].bitcast(I32), in_=w2s_hbm[r].bitcast(I32))
+        nc.sync.dma_start(out=scale_col[:], in_=u1_scale.rearrange("o (p j) -> p (o j)", j=4))
+        nc.sync.dma_start(out=w2_in[:], in_=w2_words[0])
+        load_u(0)
+        load_h(0)
         load_u(1)
         load_g(0)
-        load_h(1)
         nc.sync.dma_start(out=b2_col[:], in_=b2_1.rearrange("(p t) -> p t", t=4))
         load_u(2)
+        load_h(1)
+        nc.sync.dma_start(out=bo_cls[:], in_=b_out.rearrange("(c p) -> p c", c=2))
         load_g(1)
         nc.sync.dma_start(out=bo_col[:], in_=b_out.rearrange("(p t) -> p t", t=2))
         nc.sync.dma_start(out=wo[:], in_=wo_words.rearrange("g p n -> p g n"))
@@ -131,18 +130,15 @@ def tile_gin_pc_w4_kernel(
 
         nc.scalar.activation(out=warm[:], in_=warm[:], func=EXP)
 
-        def dummies(bank, k):
-            for n in range(k):
-                nc.tensor.matmul(bank, lhsT=ident[:], rhs=ident[:], start=True, stop=True)
-
         def spread_scale():
             bank = tr_pool.tile([P, 4, P], F32, name="bank", tag="tr")
-            dummies(bank[:, 0, :], 4)
             for j in range(4):
                 nc.tensor.transpose(bank[:, j, :], scale_col[:, j : j + 1].to_broadcast([P, P]), ident[:])
-            nc.scalar.copy(
-                out=scale_all[:].rearrange("p (n j) -> p n j", j=4), in_=bank[:].rearrange("p j n -> p n j")
-            )
+            for c in range(2):
+                nc.scalar.copy(
+                    out=scale_all[:, c, :].rearrange("p (n j) -> p n j", j=4),
+                    in_=bank[:].rearrange("p j n -> p n j"),
+                )
 
         def spread_b_out():
             bank = tr_pool.tile([P, P], F32, name="bank", tag="tr")
@@ -161,22 +157,41 @@ def tile_gin_pc_w4_kernel(
                 in_=w2s_in[:].rearrange("p (m t) -> p t m", t=4),
             )
 
-        def widen(i):
-            for b in range(2):
-                nc.vector.tensor_tensor(
-                    out=u_val[i][:, b, :], in0=block(u_raw, 2 * i + b).bitcast(FP8), in1=scale_all[:], op=MULT
-                )
+        def widen(i, b):
+            nc.vector.tensor_tensor(
+                out=u_val[i][:, b, :], in0=block(u_raw, 2 * i + b).bitcast(FP8), in1=scale_all[:, 0, :], op=MULT
+            )
 
-        def turn(src, dst, k=1):
+        def widen_pair(i):
+            c = min(i, 2)
+            b0 = 2 * i - chunks[c][0]
+            nc.vector.tensor_tensor(
+                out=u_val[i][:].rearrange("p b k -> p (b k)"),
+                in0=u_raw[c][:, b0 : b0 + 2, :].rearrange("p b k -> p (b k)").bitcast(FP8),
+                in1=scale_all[:].rearrange("p b k -> p (b k)"),
+                op=MULT,
+            )
+
+        banks = {}
+
+        def source(x, i, b):
+            if x == "u":
+                return u_val[i][:, b, :]
+            return block(h_sb if x == "h" else g_sb, 2 * i + b)
+
+        def turn(x, i):
             bank = tr_pool.tile([P, 2, 2, P], F32, name="bank", tag="tr")
-            dummies(bank[:, 0, 0, :], k)
+            banks[x, i] = bank
             for b in range(2):
-                words = src[b].bitcast(F32)
+                words = source(x, i, b).bitcast(F32)
                 for e in range(2):
                     nc.tensor.transpose(bank[:, b, e, :], words[:, e : HID // 2 : 2], ident[:])
+
+        def group(x, i):
+            dst = u_grp[i][:] if x == "u" else hg_grp[i][:, 0 if x == "h" else 1]
             nc.scalar.copy(
                 out=dst.rearrange("p (b n) t -> p b n t", b=2).bitcast(F32),
-                in_=bank[:].rearrange("p b e n -> p b n e"),
+                in_=banks[x, i][:].rearrange("p b e n -> p b n e"),
             )
 
         def quantize(codes, scl, grp):
@@ -191,208 +206,247 @@ def tile_gin_pc_w4_kernel(
         def quantize_h2(i):
             quantize(h2_codes[i], h2_scl[i], h2_grp[i][:].rearrange("p n t -> p (n t)"))
 
-        h2_ps = {}
-
-        def matmul_h2(i):
-            for b in range(2):
-                bank = h2_pool.tile([P, 4, P], F32, name="h2_bank", tag="h2")
-                h2_ps[i, b] = bank
-                nodes = slice(b * P, (b + 1) * P)
-                for t in range(4):
-                    nc.tensor.matmul_mx(
-                        out=bank[:, t, :],
-                        lhsT=w2_perm[:, 2 * P * t : 2 * P * (t + 1)].bitcast(FP4X4),
-                        lhsT_scale=w2s_perm[:, P * t : P * (t + 1)],
-                        rhs=u_codes[i][:, nodes].bitcast(FP8X4),
-                        rhs_scale=u_scl[i][:, nodes],
-                        start=True,
-                        stop=True,
-                    )
-
-        def bias_h2(i):
-            for b in range(2):
-                nc.vector.tensor_tensor(
-                    out=h2_grp[i][:, b * P : (b + 1) * P, :],
-                    in0=h2_ps[i, b][:].rearrange("p t n -> p n t"),
-                    in1=b2_col[:].unsqueeze(1).to_broadcast([P, P, 4]),
-                    op=ADD,
+        def matmul_h2(i, b):
+            bank = h2_pool.tile([P, 4, P], F32, name="h2_bank", tag="h2")
+            banks["h2", i, b] = bank
+            nodes = slice(b * P, (b + 1) * P)
+            for t in range(4):
+                nc.tensor.matmul_mx(
+                    out=bank[:, t, :],
+                    lhsT=w2_perm[:, 2 * P * t : 2 * P * (t + 1)].bitcast(FP4X4),
+                    lhsT_scale=w2s_perm[:, P * t : P * (t + 1)],
+                    rhs=u_codes[i][:, nodes].bitcast(FP8X4),
+                    rhs_scale=u_scl[i][:, nodes],
+                    start=True,
+                    stop=True,
                 )
 
-        lg_ps = {}
-
-        def matmul_out(i):
-            bank = lg_pool.tile([P, 2, CLS], F32, name="lg_bank", tag="lg")
-            lg_ps[i] = bank
-            for b in range(2):
-                for c in range(2):
-                    cls = slice(c * P, (c + 1) * P)
-                    for g in range(3):
-                        if g < 2:
-                            n0 = g * 256 + b * P
-                            codes, scl = hg_codes[i], hg_scl[i]
-                        else:
-                            n0 = b * P
-                            codes, scl = h2_codes[i], h2_scl[i]
-                        nc.tensor.matmul_mx(
-                            out=bank[:, b, cls],
-                            lhsT=codes[:, n0 : n0 + P].bitcast(FP8X4),
-                            lhsT_scale=scl[:, n0 : n0 + P],
-                            rhs=wo[:, g, 2 * P * c : 2 * P * (c + 1)].bitcast(FP4X4),
-                            rhs_scale=wos[:, g, cls],
-                            start=(g == 0),
-                            stop=(g == 2),
-                        )
-
-        def bias_out(i, blocks=slice(0, 2)):
-            k = blocks.stop - blocks.start
+        def bias_h2(i, b):
             nc.vector.tensor_tensor(
-                out=logits[i][:, blocks, :],
-                in0=lg_ps[i][:, blocks, :],
-                in1=bo_all[:].unsqueeze(1).to_broadcast([P, k, CLS]),
+                out=h2_grp[i][:, b * P : (b + 1) * P, :],
+                in0=banks["h2", i, b][:].rearrange("p t n -> p n t"),
+                in1=b2_col[:].unsqueeze(1).to_broadcast([P, P, 4]),
                 op=ADD,
             )
 
-        def row_max(i, blocks=slice(0, 2)):
+        def bias_h2_scalar(i, b):
+            for t in range(4):
+                nc.scalar.activation(
+                    out=h2_flat[i][:, b, t, :],
+                    in_=banks["h2", i, b][:, t, :],
+                    func=IDENT,
+                    bias=b2_col[:, t : t + 1],
+                )
+
+        def interleave_h2(i, b):
+            nc.vector.tensor_copy(
+                out=h2_grp[i][:, b * P : (b + 1) * P, :], in_=h2_flat[i][:, b].rearrange("p t n -> p n t")
+            )
+
+        def cat_codes(i, g, b):
+            n0 = (g * 256 if g < 2 else 0) + b * P
+            codes, scl = (hg_codes[i], hg_scl[i]) if g < 2 else (h2_codes[i], h2_scl[i])
+            return codes[:, n0 : n0 + P].bitcast(FP8X4), scl[:, n0 : n0 + P]
+
+        def wo_codes(g, c):
+            return wo[:, g, 2 * P * c : 2 * P * (c + 1)].bitcast(FP4X4), wos[:, g, c * P : (c + 1) * P]
+
+        def matmul_out(i):
+            bank = tr_pool.tile([P, 2, CLS], F32, name="bank", tag="tr")
+            banks["lg", i] = bank
+            for b in range(2):
+                for c in range(2):
+                    for g in range(3):
+                        x, xs = cat_codes(i, g, b)
+                        w, ws = wo_codes(g, c)
+                        nc.tensor.matmul_mx(
+                            out=bank[:, b, c * P : (c + 1) * P],
+                            lhsT=x, lhsT_scale=xs, rhs=w, rhs_scale=ws,
+                            start=(g == 0), stop=(g == 2),
+                        )
+
+        def matmul_out_t(i):
+            bank = lgt_pool.tile([P, 2, 2, P], F32, name="lgt_bank", tag="lgt")
+            banks["lgt", i] = bank
+            for c in range(2):
+                for b in range(2):
+                    for g in range(3):
+                        x, xs = cat_codes(i, g, b)
+                        w, ws = wo_codes(g, c)
+                        nc.tensor.matmul_mx(
+                            out=bank[:, c, b, :],
+                            lhsT=w, lhsT_scale=ws, rhs=x, rhs_scale=xs,
+                            start=(g == 0), stop=(g == 2),
+                        )
+
+        def bias_out_t(i):
+            for c in range(2):
+                nc.scalar.activation(
+                    out=lgt_sb[i][:, c, :],
+                    in_=banks["lgt", i][:, c].rearrange("p b n -> p (b n)"),
+                    func=IDENT,
+                    bias=bo_cls[:, c : c + 1],
+                )
+
+        def turn_back(i):
+            if i in LGB:
+                bank = lgb_pool.tile([P, 2, CLS], F32, name="lgb_bank", tag="lgb")
+            else:
+                bank = tr_pool.tile([P, 2, CLS], F32, name="bank", tag="tr")
+            banks["lgb", i] = bank
+            for b in range(2):
+                for c in range(2):
+                    nc.tensor.transpose(
+                        bank[:, b, c * P : (c + 1) * P], lgt_sb[i][:, c, b * P : (b + 1) * P], ident[:]
+                    )
+
+        def logit_rows(i):
+            return banks["lgb", i] if ("lgb", i) in banks else logits[i]
+
+        def bias_out(i, blocks=BOTH):
+            nc.vector.tensor_tensor(
+                out=logits[i][:, blocks, :],
+                in0=banks["lg", i][:, blocks, :],
+                in1=bo_all[:].unsqueeze(1).to_broadcast([P, blocks.stop - blocks.start, CLS]),
+                op=ADD,
+            )
+
+        def row_max(i, blocks=BOTH):
             nc.vector.tensor_reduce(
                 out=nmax[:, 2 * i + blocks.start : 2 * i + blocks.stop],
-                in_=logits[i][:, blocks, :],
+                in_=logit_rows(i)[:, blocks, :],
                 axis=AX,
                 op=MAX,
                 negate=True,
             )
 
-        def exp_sum(i, blocks=slice(0, 2)):
-            for b in range(blocks.start, blocks.stop):
-                n = 2 * i + b
-                nc.scalar.activation(
-                    out=junk[:],
-                    in_=logits[i][:, b, :],
-                    func=EXP,
-                    bias=nmax[:, n : n + 1],
-                    accum_out=ssum[:, n : n + 1],
-                )
+        def exp_sum(i, b):
+            n = 2 * i + b
+            nc.scalar.activation(
+                out=junk[:],
+                in_=logit_rows(i)[:, b, :],
+                func=EXP,
+                bias=nmax[:, n : n + 1],
+                accum_out=ssum[:, n : n + 1],
+            )
 
         def log_sum(b0, b1):
             nc.scalar.activation(out=lns[:, b0:b1], in_=ssum[:, b0:b1], func=LN)
 
-        def make_shift(b0, b1):
-            nc.vector.tensor_tensor(out=shift[:, b0:b1], in0=nmax[:, b0:b1], in1=lns[:, b0:b1], op=SUB)
-
-        def gpsimd_shift(i):
-            cols = slice(2 * i, 2 * i + 2)
-            root = sb([P, 2], F32, f"root{i}")
-            den = sb([P, 2], F32, f"den{i}")
-            z = sb([P, 2], F32, f"z{i}")
-            w = sb([P, 2], F32, f"w{i}")
-            q = sb([P, 2], F32, f"q{i}")
-            g = nc.gpsimd
-            g.tensor_tensor(out=root[:], in0=ssum[:, cols], in1=root_exp[:], op=POW)
-            g.tensor_scalar(out=den[:], in0=root[:], scalar1=LOG_MID, scalar2=None, op0=ADD)
-            g.tensor_tensor(out=den[:], in0=den[:], in1=minus_one[:], op=POW)
-            g.tensor_scalar(out=root[:], in0=root[:], scalar1=-LOG_MID, scalar2=None, op0=ADD)
-            g.tensor_tensor(out=z[:], in0=root[:], in1=den[:], op=MULT)
-            g.tensor_tensor(out=w[:], in0=z[:], in1=z[:], op=MULT)
-            g.tensor_scalar(out=q[:], in0=w[:], scalar1=1.0 / 5.0, scalar2=1.0 / 3.0, op0=MULT, op1=ADD)
-            g.tensor_tensor(out=q[:], in0=q[:], in1=w[:], op=MULT)
-            g.tensor_tensor(out=q[:], in0=q[:], in1=z[:], op=MULT)
-            g.tensor_tensor(out=q[:], in0=q[:], in1=z[:], op=ADD)
-            g.tensor_scalar(
-                out=q[:], in0=q[:], scalar1=-128.0, scalar2=-64.0 * math.log(LOG_MID), op0=MULT, op1=ADD
-            )
-            g.tensor_tensor(out=shift[:, cols], in0=q[:], in1=nmax[:, cols], op=ADD)
-
-        def finish(i, b, on_scalar):
-            n = 2 * i + b
-            if on_scalar:
-                nc.scalar.activation(
-                    out=res[i][:, b, :], in_=logits[i][:, b, :], func=IDENT, bias=shift[:, n : n + 1]
-                )
-            else:
-                nc.vector.tensor_scalar(
-                    out=res[i][:, b, :], in0=logits[i][:, b, :], scalar1=shift[:, n : n + 1], scalar2=None, op0=ADD
-                )
-
-        def finish_ln(i, b):
+        def finish(i, b):
             n = 2 * i + b
             nc.vector.tensor_scalar(
                 out=res[i][:, b, :],
-                in0=logits[i][:, b, :],
+                in0=logit_rows(i)[:, b, :],
                 scalar1=nmax[:, n : n + 1],
                 scalar2=lns[:, n : n + 1],
                 op0=ADD,
                 op1=SUB,
             )
 
-        def store(i):
-            nc.sync.dma_start(out=o_hbm[:, 2 * i : 2 * i + 2, :], in_=res[i][:])
-
-        def turn_u(i):
-            turn([u_val[i][:, b, :] for b in range(2)], u_grp[i][:])
-
-        def turn_hg(i):
-            turn([block(h_sb, 2 * i + b) for b in range(2)], hg_grp[i][:, 0])
-            turn([block(g_sb, 2 * i + b) for b in range(2)], hg_grp[i][:, 1])
-
-        def turn_h(i):
-            turn([block(h_sb, 2 * i + b) for b in range(2)], hg_grp[i][:, 0])
-
-        def turn_g(i):
-            turn([block(g_sb, 2 * i + b) for b in range(2)], hg_grp[i][:, 1])
+        def store(i, b):
+            nc.sync.dma_start(out=o_hbm[:, 2 * i + b, :], in_=res[i][:, b, :])
 
         spread_scale()
-        permute_w2_words()
-        turn_h(0)
-        widen(0)
-        turn_u(0)
         permute_w2_scales()
-        widen(1)
-        turn_g(0)
-        turn_u(1)
+        turn("h", 0)
+        permute_w2_words()
+        widen(0, 0)
+        widen(0, 1)
+        widen_pair(1)
+        group("h", 0)
+        turn("u", 0)
+        group("u", 0)
+        turn("g", 0)
         quantize_u(0)
-        matmul_h2(0)
+        turn("u", 1)
+        matmul_h2(0, 1)
+        group("g", 0)
+        widen_pair(2)
         spread_b_out()
-        widen(2)
-        turn_u(2)
-        turn_h(1)
+        matmul_h2(0, 0)
+        bias_h2(0, 1)
+        bias_h2(0, 0)
+        group("u", 1)
+        turn("g", 1)
+        turn("u", 2)
         quantize_hg(0)
-        quantize_u(1)
-        bias_h2(0)
-        matmul_h2(1)
-        turn_g(1)
-        widen(3)
-        turn_u(3)
         quantize_h2(0)
-        matmul_out(0)
-        for i in range(1, NP):
-            if i + 1 < NP:
-                quantize_u(i + 1)
-            bias_h2(i)
-            if i + 1 < NP:
-                matmul_h2(i + 1)
-                turn_hg(i + 1)
-            quantize_hg(i)
-            bias_out(i - 1)
-            quantize_h2(i)
-            matmul_out(i)
-            row_max(i - 1)
-            exp_sum(i - 1)
-            if i < 3:
-                gpsimd_shift(i - 1)
-        last = NP - 1
-        for b in range(2):
-            blk = slice(b, b + 1)
-            bias_out(last, blk)
-            row_max(last, blk)
-            exp_sum(last, blk)
-        for i in range(2):
-            finish(i, 0, False)
-            finish(i, 1, False)
-            store(i)
-        log_sum(4, 8)
-        finish_ln(2, 0)
-        make_shift(4, 8)
-        finish(2, 1, True)
-        store(2)
-        finish_ln(3, 0)
-        finish_ln(3, 1)
-        store(3)
+        quantize_u(1)
+        turn("h", 1)
+        group("u", 2)
+        matmul_out_t(0)
+        matmul_h2(1, 1)
+        group("h", 1)
+        matmul_h2(1, 0)
+        group("g", 1)
+        quantize_u(2)
+        bias_out_t(0)
+        turn("h", 2)
+        turn_back(0)
+        widen_pair(3)
+        quantize_hg(1)
+        turn("u", 3)
+        turn("g", 2)
+        bias_h2(1, 1)
+        row_max(0)
+        group("h", 2)
+        bias_h2(1, 0)
+        group("u", 3)
+        matmul_h2(2, 1)
+        quantize_u(3)
+        exp_sum(0, 0)
+        exp_sum(0, 1)
+        matmul_h2(2, 0)
+        turn("h", 3)
+        quantize_h2(1)
+        group("g", 2)
+        turn("g", 3)
+        bias_h2(2, 1)
+        log_sum(0, 2)
+        group("h", 3)
+        group("g", 3)
+        matmul_h2(3, 0)
+        bias_h2(2, 0)
+        quantize_hg(2)
+        bias_h2(3, 0)
+        matmul_h2(3, 1)
+        matmul_out_t(1)
+        quantize_h2(2)
+        bias_out_t(1)
+        bias_h2(3, 1)
+        quantize_hg(3)
+        quantize_h2(3)
+        matmul_out(2)
+        turn_back(1)
+        matmul_out(3)
+        bias_out(2, slice(0, 2))
+        row_max(1)
+        exp_sum(1, 0)
+        exp_sum(1, 1)
+        row_max(2, slice(0, 2))
+        bias_out(3, slice(1, 2))
+        bias_out(3, slice(0, 1))
+        row_max(3, slice(1, 2))
+        row_max(3, slice(0, 1))
+        exp_sum(2, 0)
+        exp_sum(2, 1)
+        finish(0, 1)
+        exp_sum(3, 1)
+        exp_sum(3, 0)
+        log_sum(2, 8)
+        finish(0, 0)
+        finish(3, 1)
+        finish(3, 0)
+        finish(1, 1)
+        store(0, 0)
+        finish(2, 1)
+        store(0, 1)
+        store(3, 1)
+        store(3, 0)
+        finish(2, 0)
+        store(1, 1)
+        finish(1, 0)
+        store(2, 0)
+        store(1, 0)
+        store(2, 1)

@@ -20,14 +20,12 @@ MAX = mybir.AluOpType.max
 AX = mybir.AxisListType.X
 EXP = mybir.ActivationFunctionType.Exp
 LN = mybir.ActivationFunctionType.Ln
-IDENT = mybir.ActivationFunctionType.Identity
 
 P = 128
 NODES, HID, CLS = 1024, 512, 256
 NB = NODES // P
 NP = NB // 2
 BOTH = slice(0, 2)
-LGB = (0, 1)
 
 
 def tile_gin_pc_w4_kernel(
@@ -36,10 +34,9 @@ def tile_gin_pc_w4_kernel(
     nc = tc.nc
     with ExitStack() as ctx:
         keep = ctx.enter_context(tc.tile_pool(name="keep", bufs=1))
-        tr_pool = ctx.enter_context(tc.psum_pool(name="tr_pool", bufs=3))
+        tr_pool = ctx.enter_context(tc.psum_pool(name="tr_pool", bufs=4))
         h2_pool = ctx.enter_context(tc.psum_pool(name="h2_pool", bufs=2))
-        lgt_pool = ctx.enter_context(tc.psum_pool(name="lgt_pool", bufs=1))
-        lgb_pool = ctx.enter_context(tc.psum_pool(name="lgb_pool", bufs=2))
+        lg_pool = ctx.enter_context(tc.psum_pool(name="lg_pool", bufs=2))
         ctx.enter_context(tc.manual_schedule())
 
         def sb(shape, dtype, name):
@@ -47,7 +44,6 @@ def tile_gin_pc_w4_kernel(
 
         scale_col = sb([P, 4], F32, "scale_col")
         bo_col = sb([P, 2], BF16, "bo_col")
-        bo_cls = sb([P, 2], BF16, "bo_cls")
         b2_col = sb([P, 4], BF16, "b2_col")
         chunks = [(0, 2), (2, 4), (4, 8)]
         u_raw = [sb([P, b1 - b0, HID], U8, f"u_raw{b0}") for b0, b1 in chunks]
@@ -70,7 +66,6 @@ def tile_gin_pc_w4_kernel(
         u_val = [sb([P, 2, HID], BF16, f"u_val{i}") for i in range(NP)]
         u_grp = [sb([P, 256, 4], BF16, f"u_grp{i}") for i in range(NP)]
         hg_grp = [sb([P, 2, 256, 4], BF16, f"hg_grp{i}") for i in range(NP)]
-        h2_flat = [sb([P, 2, 4, P], BF16, f"h2_flat{i}") for i in range(NP)]
         h2_grp = [sb([P, 256, 4], BF16, f"h2_grp{i}") for i in range(NP)]
         u_codes = [sb([P, 256], U32, f"u_codes{i}") for i in range(NP)]
         u_scl = [sb([P, 256], U8, f"u_scl{i}") for i in range(NP)]
@@ -79,7 +74,6 @@ def tile_gin_pc_w4_kernel(
         h2_codes = [sb([P, 256], U32, f"h2_codes{i}") for i in range(NP)]
         h2_scl = [sb([P, 256], U8, f"h2_scl{i}") for i in range(NP)]
         logits = [sb([P, 2, CLS], F32, f"logits{i}") for i in range(NP)]
-        lgt_sb = [sb([P, 2, 256], F32, f"lgt_sb{i}") for i in range(NP)]
         junk = sb([P, CLS], F32, "junk")
         nmax = sb([P, NB], F32, "nmax")
         ssum = sb([P, NB], F32, "ssum")
@@ -118,7 +112,6 @@ def tile_gin_pc_w4_kernel(
         nc.sync.dma_start(out=b2_col[:], in_=b2_1.rearrange("(p t) -> p t", t=4))
         load_u(2)
         load_h(1)
-        nc.sync.dma_start(out=bo_cls[:], in_=b_out.rearrange("(c p) -> p c", c=2))
         load_g(1)
         nc.sync.dma_start(out=bo_col[:], in_=b_out.rearrange("(p t) -> p t", t=2))
         nc.sync.dma_start(out=wo[:], in_=wo_words.rearrange("g p n -> p g n"))
@@ -229,20 +222,6 @@ def tile_gin_pc_w4_kernel(
                 op=ADD,
             )
 
-        def bias_h2_scalar(i, b):
-            for t in range(4):
-                nc.scalar.activation(
-                    out=h2_flat[i][:, b, t, :],
-                    in_=banks["h2", i, b][:, t, :],
-                    func=IDENT,
-                    bias=b2_col[:, t : t + 1],
-                )
-
-        def interleave_h2(i, b):
-            nc.vector.tensor_copy(
-                out=h2_grp[i][:, b * P : (b + 1) * P, :], in_=h2_flat[i][:, b].rearrange("p t n -> p n t")
-            )
-
         def cat_codes(i, g, b):
             n0 = (g * 256 if g < 2 else 0) + b * P
             codes, scl = (hg_codes[i], hg_scl[i]) if g < 2 else (h2_codes[i], h2_scl[i])
@@ -252,7 +231,7 @@ def tile_gin_pc_w4_kernel(
             return wo[:, g, 2 * P * c : 2 * P * (c + 1)].bitcast(FP4X4), wos[:, g, c * P : (c + 1) * P]
 
         def matmul_out(i):
-            bank = tr_pool.tile([P, 2, CLS], F32, name="bank", tag="tr")
+            bank = lg_pool.tile([P, 2, CLS], F32, name="lg_bank", tag="lg")
             banks["lg", i] = bank
             for b in range(2):
                 for c in range(2):
@@ -265,44 +244,6 @@ def tile_gin_pc_w4_kernel(
                             start=(g == 0), stop=(g == 2),
                         )
 
-        def matmul_out_t(i):
-            bank = lgt_pool.tile([P, 2, 2, P], F32, name="lgt_bank", tag="lgt")
-            banks["lgt", i] = bank
-            for c in range(2):
-                for b in range(2):
-                    for g in range(3):
-                        x, xs = cat_codes(i, g, b)
-                        w, ws = wo_codes(g, c)
-                        nc.tensor.matmul_mx(
-                            out=bank[:, c, b, :],
-                            lhsT=w, lhsT_scale=ws, rhs=x, rhs_scale=xs,
-                            start=(g == 0), stop=(g == 2),
-                        )
-
-        def bias_out_t(i):
-            for c in range(2):
-                nc.scalar.activation(
-                    out=lgt_sb[i][:, c, :],
-                    in_=banks["lgt", i][:, c].rearrange("p b n -> p (b n)"),
-                    func=IDENT,
-                    bias=bo_cls[:, c : c + 1],
-                )
-
-        def turn_back(i):
-            if i in LGB:
-                bank = lgb_pool.tile([P, 2, CLS], F32, name="lgb_bank", tag="lgb")
-            else:
-                bank = tr_pool.tile([P, 2, CLS], F32, name="bank", tag="tr")
-            banks["lgb", i] = bank
-            for b in range(2):
-                for c in range(2):
-                    nc.tensor.transpose(
-                        bank[:, b, c * P : (c + 1) * P], lgt_sb[i][:, c, b * P : (b + 1) * P], ident[:]
-                    )
-
-        def logit_rows(i):
-            return banks["lgb", i] if ("lgb", i) in banks else logits[i]
-
         def bias_out(i, blocks=BOTH):
             nc.vector.tensor_tensor(
                 out=logits[i][:, blocks, :],
@@ -314,7 +255,7 @@ def tile_gin_pc_w4_kernel(
         def row_max(i, blocks=BOTH):
             nc.vector.tensor_reduce(
                 out=nmax[:, 2 * i + blocks.start : 2 * i + blocks.stop],
-                in_=logit_rows(i)[:, blocks, :],
+                in_=logits[i][:, blocks, :],
                 axis=AX,
                 op=MAX,
                 negate=True,
@@ -324,7 +265,7 @@ def tile_gin_pc_w4_kernel(
             n = 2 * i + b
             nc.scalar.activation(
                 out=junk[:],
-                in_=logit_rows(i)[:, b, :],
+                in_=logits[i][:, b, :],
                 func=EXP,
                 bias=nmax[:, n : n + 1],
                 accum_out=ssum[:, n : n + 1],
@@ -337,7 +278,7 @@ def tile_gin_pc_w4_kernel(
             n = 2 * i + b
             nc.vector.tensor_scalar(
                 out=res[i][:, b, :],
-                in0=logit_rows(i)[:, b, :],
+                in0=logits[i][:, b, :],
                 scalar1=nmax[:, n : n + 1],
                 scalar2=lns[:, n : n + 1],
                 op0=ADD,
@@ -349,104 +290,102 @@ def tile_gin_pc_w4_kernel(
 
         spread_scale()
         permute_w2_scales()
-        turn("h", 0)
         permute_w2_words()
         widen(0, 0)
         widen(0, 1)
-        widen_pair(1)
+        turn("h", 0)
         group("h", 0)
+        widen_pair(1)
         turn("u", 0)
         group("u", 0)
         turn("g", 0)
-        quantize_u(0)
-        turn("u", 1)
-        matmul_h2(0, 1)
+        widen_pair(3)
         group("g", 0)
-        widen_pair(2)
-        spread_b_out()
-        matmul_h2(0, 0)
-        bias_h2(0, 1)
-        bias_h2(0, 0)
+        turn("u", 1)
         group("u", 1)
-        turn("g", 1)
-        turn("u", 2)
-        quantize_hg(0)
-        quantize_h2(0)
-        quantize_u(1)
         turn("h", 1)
-        group("u", 2)
-        matmul_out_t(0)
-        matmul_h2(1, 1)
+        turn("u", 3)
         group("h", 1)
+        quantize_u(0)
+        widen_pair(2)
+        matmul_h2(0, 1)
+        bias_h2(0, 1)
+        matmul_h2(0, 0)
+        group("u", 3)
+        bias_h2(0, 0)
+        spread_b_out()
+        quantize_hg(0)
+        quantize_u(1)
+        quantize_u(3)
+        turn("u", 2)
+        turn("g", 1)
+        turn("h", 2)
+        quantize_h2(0)
         matmul_h2(1, 0)
         group("g", 1)
+        group("u", 2)
         quantize_u(2)
-        bias_out_t(0)
-        turn("h", 2)
-        turn_back(0)
-        widen_pair(3)
-        quantize_hg(1)
-        turn("u", 3)
-        turn("g", 2)
-        bias_h2(1, 1)
-        row_max(0)
-        group("h", 2)
         bias_h2(1, 0)
-        group("u", 3)
+        matmul_h2(1, 1)
+        matmul_out(0)
+        bias_h2(1, 1)
+        quantize_hg(1)
+        quantize_h2(1)
+        matmul_h2(2, 0)
+        group("h", 2)
+        bias_out(0, slice(0, 2))
+        matmul_out(1)
         matmul_h2(2, 1)
-        quantize_u(3)
+        turn("g", 2)
+        turn("h", 3)
+        turn("g", 3)
+        bias_h2(2, 0)
+        row_max(0, slice(0, 2))
+        bias_out(1, slice(0, 2))
+        bias_h2(2, 1)
         exp_sum(0, 0)
         exp_sum(0, 1)
-        matmul_h2(2, 0)
-        turn("h", 3)
-        quantize_h2(1)
-        group("g", 2)
-        turn("g", 3)
-        bias_h2(2, 1)
-        log_sum(0, 2)
-        group("h", 3)
-        group("g", 3)
         matmul_h2(3, 0)
-        bias_h2(2, 0)
+        row_max(1, slice(0, 2))
+        group("g", 2)
         quantize_hg(2)
-        bias_h2(3, 0)
+        group("h", 3)
         matmul_h2(3, 1)
-        matmul_out_t(1)
-        quantize_h2(2)
-        bias_out_t(1)
-        bias_h2(3, 1)
-        quantize_hg(3)
-        quantize_h2(3)
-        matmul_out(2)
-        turn_back(1)
-        matmul_out(3)
-        bias_out(2, slice(0, 2))
-        row_max(1)
         exp_sum(1, 0)
         exp_sum(1, 1)
+        quantize_h2(2)
+        bias_h2(3, 0)
+        group("g", 3)
+        bias_h2(3, 1)
+        quantize_hg(3)
+        matmul_out(2)
+        quantize_h2(3)
+        matmul_out(3)
+        bias_out(2, slice(0, 2))
+        log_sum(0, 4)
         row_max(2, slice(0, 2))
-        bias_out(3, slice(1, 2))
         bias_out(3, slice(0, 1))
-        row_max(3, slice(1, 2))
+        bias_out(3, slice(1, 2))
         row_max(3, slice(0, 1))
+        row_max(3, slice(1, 2))
         exp_sum(2, 0)
         exp_sum(2, 1)
-        finish(0, 1)
-        exp_sum(3, 1)
         exp_sum(3, 0)
-        log_sum(2, 8)
-        finish(0, 0)
-        finish(3, 1)
-        finish(3, 0)
-        finish(1, 1)
-        store(0, 0)
-        finish(2, 1)
-        store(0, 1)
-        store(3, 1)
-        store(3, 0)
-        finish(2, 0)
-        store(1, 1)
         finish(1, 0)
-        store(2, 0)
         store(1, 0)
+        exp_sum(3, 1)
+        finish(0, 1)
+        finish(0, 0)
+        store(0, 1)
+        store(0, 0)
+        finish(1, 1)
+        store(1, 1)
+        log_sum(4, 8)
+        finish(3, 1)
+        store(3, 1)
+        finish(2, 1)
         store(2, 1)
+        finish(2, 0)
+        finish(3, 0)
+        store(2, 0)
+        store(3, 0)

@@ -20,6 +20,7 @@ MAX = mybir.AluOpType.max
 AX = mybir.AxisListType.X
 EXP = mybir.ActivationFunctionType.Exp
 LN = mybir.ActivationFunctionType.Ln
+IDENT = mybir.ActivationFunctionType.Identity
 
 P = 128
 NODES, HID, CLS = 1024, 512, 256
@@ -45,14 +46,12 @@ def tile_gin_pc_w4_kernel(
         scale_col = sb([P, 4], F32, "scale_col")
         bo_col = sb([P, 2], BF16, "bo_col")
         b2_col = sb([P, 4], BF16, "b2_col")
-        chunks = [(0, 2), (2, 4), (4, 8)]
-        u_raw = [sb([P, b1 - b0, HID], U8, f"u_raw{b0}") for b0, b1 in chunks]
-        h_sb = [sb([P, b1 - b0, HID], BF16, f"h_sb{b0}") for b0, b1 in chunks]
-        g_sb = [sb([P, b1 - b0, HID], BF16, f"g_sb{b0}") for b0, b1 in chunks]
+        u_raw = [sb([P, 4, HID], U8, f"u_raw{c}") for c in range(2)]
+        h_sb = [sb([P, 4, HID], BF16, f"h_sb{c}") for c in range(2)]
+        g_sb = [sb([P, 4, HID], BF16, f"g_sb{c}") for c in range(2)]
 
         def block(tiles, n):
-            c = min(n // 2, 2)
-            return tiles[c][:, n - chunks[c][0], :]
+            return tiles[n // 4][:, n % 4, :]
 
         w2_in = sb([P, 2 * HID], U8, "w2_in")
         w2_perm = sb([P, 2 * HID], U8, "w2_perm")
@@ -66,6 +65,7 @@ def tile_gin_pc_w4_kernel(
         u_val = [sb([P, 2, HID], BF16, f"u_val{i}") for i in range(NP)]
         u_grp = [sb([P, 256, 4], BF16, f"u_grp{i}") for i in range(NP)]
         hg_grp = [sb([P, 2, 256, 4], BF16, f"hg_grp{i}") for i in range(NP)]
+        h2_flat = [sb([P, 4, 256], BF16, f"h2_flat{i}") for i in range(NP)]
         h2_grp = [sb([P, 256, 4], BF16, f"h2_grp{i}") for i in range(NP)]
         u_codes = [sb([P, 256], U32, f"u_codes{i}") for i in range(NP)]
         u_scl = [sb([P, 256], U8, f"u_scl{i}") for i in range(NP)]
@@ -87,39 +87,36 @@ def tile_gin_pc_w4_kernel(
         o_hbm = out.rearrange("(p b) c -> p b c", b=NB)
 
         def load_u(i):
-            nc.sync.dma_start(out=u_raw[i][:], in_=u_hbm[:, chunks[i][0] : chunks[i][1], :])
+            nc.sync.dma_start(out=u_raw[i][:], in_=u_hbm[:, 4 * i : 4 * i + 4, :])
 
         def load_h(i):
-            nc.sync.dma_start(out=h_sb[i][:], in_=h_hbm[:, chunks[i][0] : chunks[i][1], :])
+            nc.sync.dma_start(out=h_sb[i][:], in_=h_hbm[:, 4 * i : 4 * i + 4, :])
 
         def load_g(i):
-            nc.sync.dma_start(out=g_sb[i][:], in_=g_hbm[:, chunks[i][0] : chunks[i][1], :])
+            nc.sync.dma_start(out=g_sb[i][:], in_=g_hbm[:, 4 * i : 4 * i + 4, :])
 
-        nc.gpsimd.memset(w2s_in[:].bitcast(I32), 0)
-        nc.gpsimd.memset(warm[:], 0.0)
         make_identity(nc, ident[:])
-        nc.gpsimd.memset(wos[:].rearrange("p g n -> p (g n)").bitcast(I32), 0)
+        nc.vector.memset(warm[:], 0.0)
+        nc.vector.memset(w2s_in[:].bitcast(I32), 0)
+        nc.vector.memset(wos[:].rearrange("p g n -> p (g n)").bitcast(I32), 0)
 
+        nc.sync.dma_start(out=w2_in[:], in_=w2_words[0])
+        nc.sync.dma_start(out=scale_col[:], in_=u1_scale.rearrange("o (p j) -> p (o j)", j=4))
         w2s_hbm = w2_scales[0].rearrange("(q r) n -> r q n", r=4)
         for r in range(4):
             nc.sync.dma_start(out=w2s_in[r:P:32, :].bitcast(I32), in_=w2s_hbm[r].bitcast(I32))
-        nc.sync.dma_start(out=scale_col[:], in_=u1_scale.rearrange("o (p j) -> p (o j)", j=4))
-        nc.sync.dma_start(out=w2_in[:], in_=w2_words[0])
         load_u(0)
         load_h(0)
-        load_u(1)
         load_g(0)
+        load_u(1)
         nc.sync.dma_start(out=b2_col[:], in_=b2_1.rearrange("(p t) -> p t", t=4))
-        load_u(2)
         load_h(1)
         load_g(1)
-        nc.sync.dma_start(out=bo_col[:], in_=b_out.rearrange("(p t) -> p t", t=2))
         nc.sync.dma_start(out=wo[:], in_=wo_words.rearrange("g p n -> p g n"))
+        nc.sync.dma_start(out=bo_col[:], in_=b_out.rearrange("(p t) -> p t", t=2))
         wos_hbm = wo_scales.rearrange("g (q r) n -> r q g n", r=4)
         for r in range(4):
             nc.sync.dma_start(out=wos[r:P:32, :, :].bitcast(I32), in_=wos_hbm[r].bitcast(I32))
-        load_h(2)
-        load_g(2)
 
         nc.scalar.activation(out=warm[:], in_=warm[:], func=EXP)
 
@@ -156,8 +153,7 @@ def tile_gin_pc_w4_kernel(
             )
 
         def widen_pair(i):
-            c = min(i, 2)
-            b0 = 2 * i - chunks[c][0]
+            c, b0 = i // 2, 2 * (i % 2)
             nc.vector.tensor_tensor(
                 out=u_val[i][:].rearrange("p b k -> p (b k)"),
                 in0=u_raw[c][:, b0 : b0 + 2, :].rearrange("p b k -> p (b k)").bitcast(FP8),
@@ -221,6 +217,34 @@ def tile_gin_pc_w4_kernel(
                 in1=b2_col[:].unsqueeze(1).to_broadcast([P, P, 4]),
                 op=ADD,
             )
+
+        def matmul_h2_pair(i):
+            for u in range(2):
+                bank = h2_pool.tile([P, 2, 256], F32, name="h2_bank", tag="h2")
+                banks["h2", i, u] = bank
+                for v in range(2):
+                    t = 2 * u + v
+                    nc.tensor.matmul_mx(
+                        out=bank[:, v, :],
+                        lhsT=w2_perm[:, 2 * P * t : 2 * P * (t + 1)].bitcast(FP4X4),
+                        lhsT_scale=w2s_perm[:, P * t : P * (t + 1)],
+                        rhs=u_codes[i][:].bitcast(FP8X4),
+                        rhs_scale=u_scl[i][:],
+                        start=True,
+                        stop=True,
+                    )
+
+        def bias_h2_scalar(i):
+            for t in range(4):
+                nc.scalar.activation(
+                    out=h2_flat[i][:, t, :],
+                    in_=banks["h2", i, t // 2][:, t % 2, :],
+                    func=IDENT,
+                    bias=b2_col[:, t : t + 1],
+                )
+
+        def interleave_h2(i):
+            nc.vector.tensor_copy(out=h2_grp[i][:], in_=h2_flat[i][:].rearrange("p t n -> p n t"))
 
         def cat_codes(i, g, b):
             n0 = (g * 256 if g < 2 else 0) + b * P
@@ -288,104 +312,102 @@ def tile_gin_pc_w4_kernel(
         def store(i, b):
             nc.sync.dma_start(out=o_hbm[:, 2 * i + b, :], in_=res[i][:, b, :])
 
-        spread_scale()
-        permute_w2_scales()
         permute_w2_words()
+        spread_scale()
+        turn("h", 0)
+        permute_w2_scales()
         widen(0, 0)
         widen(0, 1)
-        turn("h", 0)
         group("h", 0)
         widen_pair(1)
-        turn("u", 0)
-        group("u", 0)
-        turn("g", 0)
-        widen_pair(3)
-        group("g", 0)
-        turn("u", 1)
-        group("u", 1)
         turn("h", 1)
-        turn("u", 3)
         group("h", 1)
-        quantize_u(0)
+        turn("u", 0)
         widen_pair(2)
-        matmul_h2(0, 1)
-        bias_h2(0, 1)
-        matmul_h2(0, 0)
-        group("u", 3)
-        bias_h2(0, 0)
-        spread_b_out()
-        quantize_hg(0)
-        quantize_u(1)
-        quantize_u(3)
-        turn("u", 2)
+        turn("g", 0)
+        turn("u", 1)
+        group("u", 0)
         turn("g", 1)
-        turn("h", 2)
-        quantize_h2(0)
-        matmul_h2(1, 0)
+        turn("u", 2)
+        group("u", 1)
+        quantize_u(0)
+        widen_pair(3)
         group("g", 1)
+        quantize_u(1)
+        matmul_h2(0, 1)
+        group("g", 0)
+        matmul_h2(0, 0)
+        spread_b_out()
+        bias_h2(0, 0)
+        bias_h2(0, 1)
         group("u", 2)
-        quantize_u(2)
-        bias_h2(1, 0)
-        matmul_h2(1, 1)
-        matmul_out(0)
-        bias_h2(1, 1)
-        quantize_hg(1)
-        quantize_h2(1)
-        matmul_h2(2, 0)
+        quantize_hg(0)
+        turn("h", 2)
         group("h", 2)
-        bias_out(0, slice(0, 2))
-        matmul_out(1)
-        matmul_h2(2, 1)
+        turn("u", 3)
+        group("u", 3)
+        quantize_h2(0)
+        quantize_u(3)
+        matmul_h2_pair(1)
+        quantize_u(2)
+        bias_h2_scalar(1)
+        matmul_out(0)
+        quantize_hg(1)
         turn("g", 2)
-        turn("h", 3)
-        turn("g", 3)
-        bias_h2(2, 0)
+        group("g", 2)
+        interleave_h2(1)
+        bias_out(0, slice(0, 2))
+        quantize_h2(1)
         row_max(0, slice(0, 2))
+        matmul_h2_pair(2)
+        bias_h2_scalar(2)
+        quantize_hg(2)
+        matmul_out(1)
         bias_out(1, slice(0, 2))
-        bias_h2(2, 1)
+        turn("g", 3)
+        turn("h", 3)
+        interleave_h2(2)
+        row_max(1, slice(0, 2))
         exp_sum(0, 0)
         exp_sum(0, 1)
+        quantize_h2(2)
         matmul_h2(3, 0)
-        row_max(1, slice(0, 2))
-        group("g", 2)
-        quantize_hg(2)
+        group("g", 3)
         group("h", 3)
         matmul_h2(3, 1)
-        exp_sum(1, 0)
-        exp_sum(1, 1)
-        quantize_h2(2)
+        matmul_out(2)
         bias_h2(3, 0)
-        group("g", 3)
         bias_h2(3, 1)
         quantize_hg(3)
-        matmul_out(2)
         quantize_h2(3)
-        matmul_out(3)
         bias_out(2, slice(0, 2))
-        log_sum(0, 4)
-        row_max(2, slice(0, 2))
+        exp_sum(1, 0)
+        exp_sum(1, 1)
+        matmul_out(3)
         bias_out(3, slice(0, 1))
-        bias_out(3, slice(1, 2))
-        row_max(3, slice(0, 1))
-        row_max(3, slice(1, 2))
+        row_max(2, slice(0, 2))
+        log_sum(0, 4)
         exp_sum(2, 0)
         exp_sum(2, 1)
+        row_max(3, slice(0, 1))
         exp_sum(3, 0)
-        finish(1, 0)
-        store(1, 0)
+        bias_out(3, slice(1, 2))
+        row_max(3, slice(1, 2))
         exp_sum(3, 1)
-        finish(0, 1)
         finish(0, 0)
-        store(0, 1)
+        finish(0, 1)
         store(0, 0)
+        finish(1, 0)
         finish(1, 1)
         store(1, 1)
+        store(0, 1)
+        store(1, 0)
         log_sum(4, 8)
+        finish(3, 0)
+        finish(2, 1)
+        store(3, 0)
+        finish(2, 0)
+        store(2, 1)
+        store(2, 0)
         finish(3, 1)
         store(3, 1)
-        finish(2, 1)
-        store(2, 1)
-        finish(2, 0)
-        finish(3, 0)
-        store(2, 0)
-        store(3, 0)

from contextlib import ExitStack

import concourse.mybir as mybir
from concourse.masks import make_identity

FLOPS = 2 * 1024 * 512 * 512 + 2 * 1024 * 1536 * 256

F32 = mybir.dt.float32
BF16 = mybir.dt.bfloat16
I32 = mybir.dt.int32
U32 = mybir.dt.uint32
U8 = mybir.dt.uint8
FP8 = mybir.dt.float8_e4m3fn
FP8X4 = mybir.dt.float8_e4m3fn_x4
FP4X4 = mybir.dt.float4_e2m1fn_x4
ADD = mybir.AluOpType.add
SUB = mybir.AluOpType.subtract
MULT = mybir.AluOpType.mult
MAX = mybir.AluOpType.max
AX = mybir.AxisListType.X
EXP = mybir.ActivationFunctionType.Exp
LN = mybir.ActivationFunctionType.Ln
IDENT = mybir.ActivationFunctionType.Identity

P = 128
NODES, HID, CLS = 1024, 512, 256
NB = NODES // P
NP = NB // 2
BOTH = slice(0, 2)


def tile_gin_pc_w4_kernel(
    tc, u1_bytes, u1_scale, w2_words, w2_scales, b2_1, h, h1, wo_words, wo_scales, b_out, out
):
    nc = tc.nc
    with ExitStack() as ctx:
        keep = ctx.enter_context(tc.tile_pool(name="keep", bufs=1))
        tr_pool = ctx.enter_context(tc.psum_pool(name="tr_pool", bufs=4))
        h2_pool = ctx.enter_context(tc.psum_pool(name="h2_pool", bufs=2))
        lg_pool = ctx.enter_context(tc.psum_pool(name="lg_pool", bufs=2))
        ctx.enter_context(tc.manual_schedule())

        def sb(shape, dtype, name):
            return keep.tile(shape, dtype, name=name, align_bytes=64)

        scale_col = sb([P, 4], F32, "scale_col")
        bo_col = sb([P, 2], BF16, "bo_col")
        b2_col = sb([P, 4], BF16, "b2_col")
        u_raw = [sb([P, 4, HID], U8, f"u_raw{c}") for c in range(2)]
        h_sb = [sb([P, 4, HID], BF16, f"h_sb{c}") for c in range(2)]
        g_sb = [sb([P, 4, HID], BF16, f"g_sb{c}") for c in range(2)]

        def block(tiles, n):
            return tiles[n // 4][:, n % 4, :]

        w2_in = sb([P, 2 * HID], U8, "w2_in")
        w2_perm = sb([P, 2 * HID], U8, "w2_perm")
        w2s_in = sb([P, HID], U8, "w2s_in")
        w2s_perm = sb([P, HID], U8, "w2s_perm")
        wo = sb([P, 3, 2 * CLS], U8, "wo")
        wos = sb([P, 3, CLS], U8, "wos")
        ident = sb([P, P], F32, "ident")
        scale_all = sb([P, 2, HID], F32, "scale_all")
        bo_all = sb([P, CLS], BF16, "bo_all")
        u_val = [sb([P, 2, HID], BF16, f"u_val{i}") for i in range(NP)]
        u_grp = [sb([P, 256, 4], BF16, f"u_grp{i}") for i in range(NP)]
        hg_grp = [sb([P, 2, 256, 4], BF16, f"hg_grp{i}") for i in range(NP)]
        h2_flat = [sb([P, 4, 256], BF16, f"h2_flat{i}") for i in range(NP)]
        h2_grp = [sb([P, 256, 4], BF16, f"h2_grp{i}") for i in range(NP)]
        u_codes = [sb([P, 256], U32, f"u_codes{i}") for i in range(NP)]
        u_scl = [sb([P, 256], U8, f"u_scl{i}") for i in range(NP)]
        hg_codes = [sb([P, 512], U32, f"hg_codes{i}") for i in range(NP)]
        hg_scl = [sb([P, 512], U8, f"hg_scl{i}") for i in range(NP)]
        h2_codes = [sb([P, 256], U32, f"h2_codes{i}") for i in range(NP)]
        h2_scl = [sb([P, 256], U8, f"h2_scl{i}") for i in range(NP)]
        logits = [sb([P, 2, CLS], F32, f"logits{i}") for i in range(NP)]
        junk = sb([P, CLS], F32, "junk")
        nmax = sb([P, NB], F32, "nmax")
        ssum = sb([P, NB], F32, "ssum")
        lns = sb([P, NB], F32, "lns")
        res = [sb([P, 2, CLS], F32, f"res{i}") for i in range(NP)]
        warm = sb([P, 1], F32, "warm")

        u_hbm = u1_bytes.rearrange("(p b) k -> p b k", b=NB)
        h_hbm = h.rearrange("(p b) k -> p b k", b=NB)
        g_hbm = h1.rearrange("(p b) k -> p b k", b=NB)
        o_hbm = out.rearrange("(p b) c -> p b c", b=NB)

        def load_u(i):
            nc.sync.dma_start(out=u_raw[i][:], in_=u_hbm[:, 4 * i : 4 * i + 4, :])

        def load_h(i):
            nc.sync.dma_start(out=h_sb[i][:], in_=h_hbm[:, 4 * i : 4 * i + 4, :])

        def load_g(i):
            nc.sync.dma_start(out=g_sb[i][:], in_=g_hbm[:, 4 * i : 4 * i + 4, :])

        make_identity(nc, ident[:])
        nc.vector.memset(warm[:], 0.0)
        nc.vector.memset(w2s_in[:].bitcast(I32), 0)
        nc.vector.memset(wos[:].rearrange("p g n -> p (g n)").bitcast(I32), 0)

        nc.sync.dma_start(out=w2_in[:], in_=w2_words[0])
        nc.sync.dma_start(out=scale_col[:], in_=u1_scale.rearrange("o (p j) -> p (o j)", j=4))
        w2s_hbm = w2_scales[0].rearrange("(q r) n -> r q n", r=4)
        for r in range(4):
            nc.sync.dma_start(out=w2s_in[r:P:32, :].bitcast(I32), in_=w2s_hbm[r].bitcast(I32))
        load_u(0)
        load_h(0)
        load_g(0)
        load_u(1)
        nc.sync.dma_start(out=b2_col[:], in_=b2_1.rearrange("(p t) -> p t", t=4))
        load_h(1)
        load_g(1)
        nc.sync.dma_start(out=wo[:], in_=wo_words.rearrange("g p n -> p g n"))
        nc.sync.dma_start(out=bo_col[:], in_=b_out.rearrange("(p t) -> p t", t=2))
        wos_hbm = wo_scales.rearrange("g (q r) n -> r q g n", r=4)
        for r in range(4):
            nc.sync.dma_start(out=wos[r:P:32, :, :].bitcast(I32), in_=wos_hbm[r].bitcast(I32))

        nc.scalar.activation(out=warm[:], in_=warm[:], func=EXP)

        def spread_scale():
            bank = tr_pool.tile([P, 4, P], F32, name="bank", tag="tr")
            for j in range(4):
                nc.tensor.transpose(bank[:, j, :], scale_col[:, j : j + 1].to_broadcast([P, P]), ident[:])
            for c in range(2):
                nc.scalar.copy(
                    out=scale_all[:, c, :].rearrange("p (n j) -> p n j", j=4),
                    in_=bank[:].rearrange("p j n -> p n j"),
                )

        def spread_b_out():
            bank = tr_pool.tile([P, P], F32, name="bank", tag="tr")
            nc.tensor.transpose(bank[:], bo_col[:].bitcast(F32).to_broadcast([P, P]), ident[:])
            nc.scalar.copy(out=bo_all[:].bitcast(F32), in_=bank[:])

        def permute_w2_words():
            nc.vector.tensor_copy(
                out=w2_perm[:].rearrange("p (t m b) -> p t m b", t=4, b=2),
                in_=w2_in[:].rearrange("p (m t b) -> p t m b", t=4, b=2),
            )

        def permute_w2_scales():
            nc.vector.tensor_copy(
                out=w2s_perm[:].rearrange("p (t m) -> p t m", t=4),
                in_=w2s_in[:].rearrange("p (m t) -> p t m", t=4),
            )

        def widen(i, b):
            nc.vector.tensor_tensor(
                out=u_val[i][:, b, :], in0=block(u_raw, 2 * i + b).bitcast(FP8), in1=scale_all[:, 0, :], op=MULT
            )

        def widen_pair(i):
            c, b0 = i // 2, 2 * (i % 2)
            nc.vector.tensor_tensor(
                out=u_val[i][:].rearrange("p b k -> p (b k)"),
                in0=u_raw[c][:, b0 : b0 + 2, :].rearrange("p b k -> p (b k)").bitcast(FP8),
                in1=scale_all[:].rearrange("p b k -> p (b k)"),
                op=MULT,
            )

        banks = {}

        def source(x, i, b):
            if x == "u":
                return u_val[i][:, b, :]
            return block(h_sb if x == "h" else g_sb, 2 * i + b)

        def turn(x, i):
            bank = tr_pool.tile([P, 2, 2, P], F32, name="bank", tag="tr")
            banks[x, i] = bank
            for b in range(2):
                words = source(x, i, b).bitcast(F32)
                for e in range(2):
                    nc.tensor.transpose(bank[:, b, e, :], words[:, e : HID // 2 : 2], ident[:])

        def group(x, i):
            dst = u_grp[i][:] if x == "u" else hg_grp[i][:, 0 if x == "h" else 1]
            nc.scalar.copy(
                out=dst.rearrange("p (b n) t -> p b n t", b=2).bitcast(F32),
                in_=banks[x, i][:].rearrange("p b e n -> p b n e"),
            )

        def quantize(codes, scl, grp):
            nc.vector.quantize_mx(out=codes[:].bitcast(FP8X4), scales=scl[:], in_=grp)

        def quantize_u(i):
            quantize(u_codes[i], u_scl[i], u_grp[i][:].rearrange("p n t -> p (n t)"))

        def quantize_hg(i):
            quantize(hg_codes[i], hg_scl[i], hg_grp[i][:].rearrange("p s n t -> p (s n t)"))

        def quantize_h2(i):
            quantize(h2_codes[i], h2_scl[i], h2_grp[i][:].rearrange("p n t -> p (n t)"))

        def matmul_h2(i, b):
            bank = h2_pool.tile([P, 4, P], F32, name="h2_bank", tag="h2")
            banks["h2", i, b] = bank
            nodes = slice(b * P, (b + 1) * P)
            for t in range(4):
                nc.tensor.matmul_mx(
                    out=bank[:, t, :],
                    lhsT=w2_perm[:, 2 * P * t : 2 * P * (t + 1)].bitcast(FP4X4),
                    lhsT_scale=w2s_perm[:, P * t : P * (t + 1)],
                    rhs=u_codes[i][:, nodes].bitcast(FP8X4),
                    rhs_scale=u_scl[i][:, nodes],
                    start=True,
                    stop=True,
                )

        def bias_h2(i, b):
            nc.vector.tensor_tensor(
                out=h2_grp[i][:, b * P : (b + 1) * P, :],
                in0=banks["h2", i, b][:].rearrange("p t n -> p n t"),
                in1=b2_col[:].unsqueeze(1).to_broadcast([P, P, 4]),
                op=ADD,
            )

        def matmul_h2_pair(i):
            for u in range(2):
                bank = h2_pool.tile([P, 2, 256], F32, name="h2_bank", tag="h2")
                banks["h2", i, u] = bank
                for v in range(2):
                    t = 2 * u + v
                    nc.tensor.matmul_mx(
                        out=bank[:, v, :],
                        lhsT=w2_perm[:, 2 * P * t : 2 * P * (t + 1)].bitcast(FP4X4),
                        lhsT_scale=w2s_perm[:, P * t : P * (t + 1)],
                        rhs=u_codes[i][:].bitcast(FP8X4),
                        rhs_scale=u_scl[i][:],
                        start=True,
                        stop=True,
                    )

        def bias_h2_scalar(i):
            for t in range(4):
                nc.scalar.activation(
                    out=h2_flat[i][:, t, :],
                    in_=banks["h2", i, t // 2][:, t % 2, :],
                    func=IDENT,
                    bias=b2_col[:, t : t + 1],
                )

        def interleave_h2(i):
            nc.vector.tensor_copy(out=h2_grp[i][:], in_=h2_flat[i][:].rearrange("p t n -> p n t"))

        def cat_codes(i, g, b):
            n0 = (g * 256 if g < 2 else 0) + b * P
            codes, scl = (hg_codes[i], hg_scl[i]) if g < 2 else (h2_codes[i], h2_scl[i])
            return codes[:, n0 : n0 + P].bitcast(FP8X4), scl[:, n0 : n0 + P]

        def wo_codes(g, c):
            return wo[:, g, 2 * P * c : 2 * P * (c + 1)].bitcast(FP4X4), wos[:, g, c * P : (c + 1) * P]

        def matmul_out(i):
            bank = lg_pool.tile([P, 2, CLS], F32, name="lg_bank", tag="lg")
            banks["lg", i] = bank
            for b in range(2):
                for c in range(2):
                    for g in range(3):
                        x, xs = cat_codes(i, g, b)
                        w, ws = wo_codes(g, c)
                        nc.tensor.matmul_mx(
                            out=bank[:, b, c * P : (c + 1) * P],
                            lhsT=x, lhsT_scale=xs, rhs=w, rhs_scale=ws,
                            start=(g == 0), stop=(g == 2),
                        )

        def bias_out(i, blocks=BOTH):
            nc.vector.tensor_tensor(
                out=logits[i][:, blocks, :],
                in0=banks["lg", i][:, blocks, :],
                in1=bo_all[:].unsqueeze(1).to_broadcast([P, blocks.stop - blocks.start, CLS]),
                op=ADD,
            )

        def row_max(i, blocks=BOTH):
            nc.vector.tensor_reduce(
                out=nmax[:, 2 * i + blocks.start : 2 * i + blocks.stop],
                in_=logits[i][:, blocks, :],
                axis=AX,
                op=MAX,
                negate=True,
            )

        def exp_sum(i, b):
            n = 2 * i + b
            nc.scalar.activation(
                out=junk[:],
                in_=logits[i][:, b, :],
                func=EXP,
                bias=nmax[:, n : n + 1],
                accum_out=ssum[:, n : n + 1],
            )

        def log_sum(b0, b1):
            nc.scalar.activation(out=lns[:, b0:b1], in_=ssum[:, b0:b1], func=LN)

        def finish(i, b):
            n = 2 * i + b
            nc.vector.tensor_scalar(
                out=res[i][:, b, :],
                in0=logits[i][:, b, :],
                scalar1=nmax[:, n : n + 1],
                scalar2=lns[:, n : n + 1],
                op0=ADD,
                op1=SUB,
            )

        def store(i, b):
            nc.sync.dma_start(out=o_hbm[:, 2 * i + b, :], in_=res[i][:, b, :])

        permute_w2_words()
        spread_scale()
        turn("h", 0)
        permute_w2_scales()
        widen(0, 0)
        widen(0, 1)
        group("h", 0)
        widen_pair(1)
        turn("h", 1)
        group("h", 1)
        turn("u", 0)
        widen_pair(2)
        turn("g", 0)
        turn("u", 1)
        group("u", 0)
        turn("g", 1)
        turn("u", 2)
        group("u", 1)
        quantize_u(0)
        widen_pair(3)
        group("g", 1)
        quantize_u(1)
        matmul_h2(0, 1)
        group("g", 0)
        matmul_h2(0, 0)
        spread_b_out()
        bias_h2(0, 0)
        bias_h2(0, 1)
        group("u", 2)
        quantize_hg(0)
        turn("h", 2)
        group("h", 2)
        turn("u", 3)
        group("u", 3)
        quantize_h2(0)
        quantize_u(3)
        matmul_h2_pair(1)
        quantize_u(2)
        bias_h2_scalar(1)
        matmul_out(0)
        quantize_hg(1)
        turn("g", 2)
        group("g", 2)
        interleave_h2(1)
        bias_out(0, slice(0, 2))
        quantize_h2(1)
        row_max(0, slice(0, 2))
        matmul_h2_pair(2)
        bias_h2_scalar(2)
        quantize_hg(2)
        matmul_out(1)
        bias_out(1, slice(0, 2))
        turn("g", 3)
        turn("h", 3)
        interleave_h2(2)
        row_max(1, slice(0, 2))
        exp_sum(0, 0)
        exp_sum(0, 1)
        quantize_h2(2)
        matmul_h2(3, 0)
        group("g", 3)
        group("h", 3)
        matmul_h2(3, 1)
        matmul_out(2)
        bias_h2(3, 0)
        bias_h2(3, 1)
        quantize_hg(3)
        quantize_h2(3)
        bias_out(2, slice(0, 2))
        exp_sum(1, 0)
        exp_sum(1, 1)
        matmul_out(3)
        bias_out(3, slice(0, 1))
        row_max(2, slice(0, 2))
        log_sum(0, 4)
        exp_sum(2, 0)
        exp_sum(2, 1)
        row_max(3, slice(0, 1))
        exp_sum(3, 0)
        bias_out(3, slice(1, 2))
        row_max(3, slice(1, 2))
        exp_sum(3, 1)
        finish(0, 0)
        finish(0, 1)
        store(0, 0)
        finish(1, 0)
        finish(1, 1)
        store(1, 1)
        store(0, 1)
        store(1, 0)
        log_sum(4, 8)
        finish(3, 0)
        finish(2, 1)
        store(3, 0)
        finish(2, 0)
        store(2, 1)
        store(2, 0)
        finish(3, 1)
        store(3, 1)
